import numpy as np
import ml_dtypes


def mxq(x, axis, fmt="e4m3"):
    dtype, down = {"e4m3": (ml_dtypes.float8_e4m3fn, 7), "e5m2": (ml_dtypes.float8_e5m2, 14)}[fmt]
    v = np.moveaxis(np.asarray(x, np.float32).astype(ml_dtypes.bfloat16).astype(np.float64), axis, -1)
    blocks = v.reshape(v.shape[:-1] + (-1, 32))
    amax = np.abs(blocks).max(-1, keepdims=True)
    byte = np.maximum(np.where(amax > 0, np.frexp(amax)[1] - 1 + 127, 0) - down, 1)
    scale = np.exp2(byte - 127.0)
    codes = (blocks / scale).astype(np.float32).astype(dtype).astype(np.float64)
    return np.moveaxis((codes * scale).reshape(v.shape), -1, axis)


WIDE = False


def mx_kscale(k):
    if not WIDE:
        return np.ones(k)
    levels = np.array([10, -10, 5, -5, 0])
    if k % 512:
        return np.exp2(np.random.permutation(np.resize(levels, k // 32))).repeat(32)
    a = np.empty((k // 512, 16))
    for p in range(k // 512):
        a[p, :8] = np.random.permutation(np.resize(levels, 8))
        for g in range(8):
            far = levels[np.abs(levels - a[p, g]) >= 10]
            a[p, g + 8] = far[np.random.randint(len(far))]
    return np.exp2(a.ravel()).repeat(32)


BF16 = ml_dtypes.bfloat16


def bf(x):
    return np.asarray(x, np.float32).astype(BF16)


def f64(x):
    return np.asarray(x).astype(np.float64)


B, DI, DH = 1024, 1024, 256


def sigmoid(v):
    return 1.0 / (1.0 + np.exp(-v))


def setup_inputs():
    s = mx_kscale(DI)
    n = np.random.standard_normal
    a, c = 0.7 / np.sqrt(DI), 0.7 / np.sqrt(DH)
    keep = np.random.uniform(size=B) < 0.9
    return {
        "x": bf(n((B, DI)) * s),
        "h_minors": bf(n((B, DH))),
        "c_minors": bf(n((B, DH))),
        "s0": bf(n((B, DH))),
        "s1": bf(n((B, DH))),
        "s2": bf(n((B, DH))),
        "mask": bf(keep * (0.5 + 0.5 * np.random.uniform(size=B))),
        "weight_ih": bf(n((7 * DH, DI)) * a / s),
        "bias_ih": bf(n(7 * DH) * 0.3),
        "weight_hh": bf(n((4 * DH, DH)) * c),
        "bias_hh": bf(n(4 * DH) * 0.3),
        "weight_sh0": bf(n((DH, DH)) * c),
        "bias_sh0": bf(n(DH) * 0.3),
        "weight_sh1": bf(n((DH, DH)) * c),
        "bias_sh1": bf(n(DH) * 0.3),
        "weight_sh2": bf(n((DH, DH)) * c),
        "bias_sh2": bf(n(DH) * 0.3),
    }


def reference(x, h_minors, c_minors, s0, s1, s2, mask, weight_ih, bias_ih, weight_hh, bias_hh,
              weight_sh0, bias_sh0, weight_sh1, bias_sh1, weight_sh2, bias_sh2):
    d = DH
    m = f64(mask)[:, None]

    tmp = (mxq(f64(x), 1, "e4m3") @ mxq(f64(weight_ih), 1, "e4m3").T) + f64(bias_ih)
    tmp2 = f64(h_minors) @ f64(weight_hh).T + f64(bias_hh)
    tmp3 = np.concatenate([
        f64(s0) @ f64(weight_sh0).T + f64(bias_sh0),
        f64(s1) @ f64(weight_sh1).T + f64(bias_sh1),
        f64(s2) @ f64(weight_sh2).T + f64(bias_sh2),
    ], axis=1)

    tmp_in, tmp_s = tmp[:, :4 * d], tmp[:, 4 * d:]
    pre = tmp_in + tmp2
    ifo = sigmoid(pre[:, :3 * d])
    c_hat = pre[:, 3 * d:]
    i_g, f_g, o_g = ifo[:, :d], ifo[:, d:2 * d], ifo[:, 2 * d:]

    c_t = (f_g * f64(c_minors) + i_g * np.tanh(c_hat)) * m
    tc = np.tanh(c_t) * m
    h = o_g * tc

    bg = sigmoid(tmp_s + tmp3)
    b0, b1, b2 = bg[:, :d], bg[:, d:2 * d], bg[:, 2 * d:]

    s_0 = (b0 + 1.0 - o_g) * tc
    s_1 = (b1 + 2.0 - o_g - s_0) * 0.5 * tc
    s_2 = (b2 + 3.0 - o_g - (2.0 * s_0 + s_1)) * (1.0 / 3.0) * tc

    return (h, c_t, s_0, s_1, s_2)

@@ -1,0 +1,389 @@
+from contextlib import ExitStack
+
+import concourse.mybir as mybir
+from concourse.masks import make_identity
+
+F32 = mybir.dt.float32
+BF16 = mybir.dt.bfloat16
+U32 = mybir.dt.uint32
+U8 = mybir.dt.uint8
+FP8X4 = mybir.dt.float8_e4m3fn_x4
+ACT = mybir.ActivationFunctionType
+ALU = mybir.AluOpType
+
+P = 128
+BATCH = 1024
+DI = 1024
+DH = 256
+GATES = 7 * DH
+ROW_TILES = BATCH // P
+K_PASS = 4 * P
+PASSES = DI // K_PASS
+KT = DH // P
+BANK = 512
+CHUNKS = ((0, 512), (512, 512), (1024, 512), (1536, 256))
+PLAIN_GROUPS = ((0, 512, 0), (512, 512, 0), (1024, 256, 1), (1280, 256, 2), (1536, 256, 3))
+BIAS_IN_PSUM_FROM = 4 * DH
+PLAIN_ROW_TILES = GATES // P
+CORE = (0, 1)
+SHARED = (2, 3)
+PER_BANK = 4
+PAIR = 2
+N_PAIRS = ROW_TILES // PAIR
+
+FLOPS = 2 * BATCH * (GATES * DI + 4 * DH * DH + 3 * DH * DH)
+
+
+def tile_share_lstm_cell_pa_kernel(
+    tc, x, h_minors, c_minors, s0, s1, s2, mask,
+    weight_ih, bias_ih, weight_hh, bias_hh,
+    weight_sh0, bias_sh0, weight_sh1, bias_sh1, weight_sh2, bias_sh2,
+    out_0, out_1, out_2, out_3, out_4,
+):
+    nc = tc.nc
+    with ExitStack() as ctx:
+        keep = ctx.enter_context(tc.tile_pool(name="keep", bufs=1))
+        stage = ctx.enter_context(tc.tile_pool(name="stage", bufs=2))
+        gate_pool = ctx.enter_context(tc.tile_pool(name="gate_pool", bufs=3))
+        work = ctx.enter_context(tc.tile_pool(name="work", bufs=2))
+        psum = ctx.enter_context(tc.psum_pool(name="psum", bufs=8))
+        ctx.enter_context(tc.manual_schedule())
+
+        def by_row_tile(ap):
+            return ap.rearrange("(p r) d -> p r d", r=ROW_TILES)
+
+        x_view = by_row_tile(x)
+        act_views = [by_row_tile(a) for a in (h_minors, s0, s1, s2)]
+        out_views = [by_row_tile(o) for o in (out_0, out_1, out_2, out_3, out_4)]
+
+        x_sb = keep.tile([P, ROW_TILES, DI], BF16)
+        acts_sb = keep.tile([P, 4, ROW_TILES, DH], BF16)
+        c_sb = keep.tile([P, ROW_TILES, DH], BF16)
+        wih_sb = keep.tile([P, GATES // P, DI], BF16)
+        wplain_sb = keep.tile([P, PLAIN_ROW_TILES, DH], BF16)
+        wplain_t = keep.tile([P, KT, GATES], BF16)
+        bias_rows = keep.tile([P, GATES], BF16)
+        bias_bc = keep.tile([P, BIAS_IN_PSUM_FROM], F32)
+        mask_bf = keep.tile([P, ROW_TILES], BF16)
+        mask_f = keep.tile([P, ROW_TILES], F32)
+        ident_bf = keep.tile([P, P], BF16)
+        ident_f = keep.tile([P, P], F32)
+        ones = keep.tile([P, P], BF16)
+        warm = keep.tile([P, 1], F32)
+        x_codes = keep.tile([P, ROW_TILES, PASSES, P], U32, align_bytes=64)
+        x_scales = keep.tile([P, ROW_TILES, PASSES, P], U8, align_bytes=64)
+        w_codes = [
+            keep.tile([P, PASSES, n], U32, align_bytes=64, name="w_codes%d" % j)
+            for j, (c0, n) in enumerate(CHUNKS)
+        ]
+        w_scales = [
+            keep.tile([P, PASSES, n], U8, align_bytes=64, name="w_scales%d" % j)
+            for j, (c0, n) in enumerate(CHUNKS)
+        ]
+
+        nc.vector.memset(warm[:], 0.0)
+        nc.vector.memset(bias_rows[:], 0.0)
+        nc.vector.memset(ones[:], 1.0)
+        make_identity(nc, ident_bf[:])
+
+        def as_row(vec):
+            return vec.rearrange("(o n) -> o n", o=1)
+
+        nc.scalar.dma_start(out=bias_rows[0:1, :], in_=as_row(bias_ih))
+        nc.scalar.dma_start(out=bias_rows[1:2, 0 : 4 * DH], in_=as_row(bias_hh))
+        for j, b in enumerate((bias_sh0, bias_sh1, bias_sh2)):
+            nc.gpsimd.dma_start(out=bias_rows[1:2, (4 + j) * DH : (5 + j) * DH], in_=as_row(b))
+        nc.gpsimd.dma_start(out=mask_bf[:], in_=mask.rearrange("(p r) -> p r", r=ROW_TILES))
+        make_identity(nc, ident_f[:])
+        nc.scalar.activation(out=warm[:], in_=warm[:], func=ACT.Sigmoid)
+
+        def load_weight_chunk(j):
+            c0, n = CHUNKS[j]
+            nc.sync.dma_start(
+                out=wih_sb[:, c0 // P : (c0 + n) // P, :],
+                in_=weight_ih[c0 : c0 + n, :].rearrange("(t p) k -> p t k", p=P),
+            )
+
+        def load_rows(first, count):
+            rows = slice(first, first + count)
+            for s in range(4):
+                nc.sync.dma_start(out=acts_sb[:, s, rows, :], in_=act_views[s][:, rows, :])
+            nc.sync.dma_start(out=x_sb[:, rows, :], in_=x_view[:, rows, :])
+
+        nc.sync.dma_start(
+            out=wplain_sb[:, 0:8, :], in_=weight_hh.rearrange("(t p) k -> p t k", p=P)
+        )
+        for j, w in enumerate((weight_sh0, weight_sh1, weight_sh2)):
+            nc.sync.dma_start(
+                out=wplain_sb[:, 8 + 2 * j : 10 + 2 * j, :],
+                in_=w.rearrange("(t p) k -> p t k", p=P),
+            )
+        load_rows(0, 2)
+        load_weight_chunk(0)
+        load_weight_chunk(1)
+        nc.sync.dma_start(out=c_sb[:], in_=by_row_tile(c_minors))
+        load_weight_chunk(2)
+        load_weight_chunk(3)
+        load_rows(2, 2)
+        load_rows(4, 4)
+
+        def copy_out(turn, out, in_):
+            if turn % 2 == 0:
+                nc.scalar.copy(out=out, in_=in_)
+            else:
+                nc.vector.tensor_copy(out=out, in_=in_)
+
+        def transpose_plain_weights():
+            turn = 0
+            for t0 in range(0, PLAIN_ROW_TILES, PER_BANK):
+                count = min(PER_BANK, PLAIN_ROW_TILES - t0)
+                for kt in range(KT):
+                    bank = psum.tile([P, PER_BANK, P], BF16, name="bank_w", tag="bank")
+                    for t in range(count):
+                        nc.tensor.transpose(
+                            bank[:, t, :], wplain_sb[:, t0 + t, kt * P : (kt + 1) * P], ident_bf[:]
+                        )
+                    copy_out(
+                        turn,
+                        wplain_t[:, kt, t0 * P : (t0 + count) * P],
+                        bank[:, 0:count, :].rearrange("p t n -> p (t n)"),
+                    )
+                    turn += 1
+
+        def broadcast_bias():
+            for c0, n in CHUNKS:
+                if c0 < BIAS_IN_PSUM_FROM:
+                    acc = psum.tile([P, BANK], F32, name="acc_bias", tag="bank")
+                    nc.tensor.matmul(
+                        acc[:, 0:n], lhsT=ones[:], rhs=bias_rows[:, c0 : c0 + n], start=True, stop=True
+                    )
+                    nc.vector.tensor_copy(out=bias_bc[:, c0 : c0 + n], in_=acc[:, 0:n])
+
+        def regroup(turn, rows_bf16, grouped_words):
+            words = rows_bf16.bitcast(F32)
+            bank = psum.tile([P, 2 * PASSES, P], F32, name="bank_q", tag="bank")
+            for g in range(PASSES):
+                for u in range(2):
+                    nc.tensor.transpose(
+                        bank[:, 2 * g + u, :], words[:, 2 * P * g + u : 2 * P * (g + 1) : 2], ident_f[:]
+                    )
+            copy_out(turn, grouped_words, bank[:].rearrange("p (g u) n -> p g n u", u=2))
+
+        w_grouped_of = {}
+
+        def regroup_weight_chunk(j):
+            c0, n = CHUNKS[j]
+            grouped = stage.tile(
+                [P, PASSES, n, 4], BF16, align_bytes=64, name="w_grouped", tag="w_grouped"
+            )
+            w_grouped_of[j] = grouped
+            grouped_words = grouped[:].bitcast(F32)
+            for t in range(n // P):
+                regroup(t, wih_sb[:, c0 // P + t, :], grouped_words[:, :, t * P : (t + 1) * P, :])
+
+        def quantise_weight_chunk(j):
+            nc.vector.quantize_mx(
+                out=w_codes[j][:].rearrange("p g n -> p (g n)").bitcast(FP8X4),
+                scales=w_scales[j][:].rearrange("p g n -> p (g n)"),
+                in_=w_grouped_of[j][:].rearrange("p g n t -> p (g n t)"),
+            )
+
+        x_grouped_of = {}
+        acts_t_of = {}
+
+        def prepare_rows(r):
+            acts_t_of[r] = stage.tile([P, 4, KT, P], BF16, name="acts_t", bufs=2 * PAIR)
+            for first in range(0, 4, PER_BANK // KT):
+                bank = psum.tile([P, PER_BANK // KT, KT, P], BF16, name="bank_a", tag="bank")
+                for s in range(PER_BANK // KT):
+                    for kt in range(KT):
+                        nc.tensor.transpose(
+                            bank[:, s, kt, :], acts_sb[:, first + s, r, kt * P : (kt + 1) * P], ident_bf[:]
+                        )
+                nc.scalar.copy(out=acts_t_of[r][:, first : first + PER_BANK // KT, :, :], in_=bank[:])
+            q, i = divmod(r, PAIR)
+            if i == 0:
+                x_grouped_of[q] = stage.tile(
+                    [P, PAIR, PASSES, P, 4], BF16, align_bytes=64, name="x_grouped"
+                )
+            regroup(0, x_sb[:, r, :], x_grouped_of[q][:].bitcast(F32)[:, i, :, :, :])
+
+        def rows_of(q):
+            return slice(q * PAIR, (q + 1) * PAIR)
+
+        def quantise_x(q):
+            nc.vector.quantize_mx(
+                out=x_codes[:, rows_of(q), :, :].rearrange("p r g b -> p (r g b)").bitcast(FP8X4),
+                scales=x_scales[:, rows_of(q), :, :].rearrange("p r g b -> p (r g b)"),
+                in_=x_grouped_of[q][:].rearrange("p r g b t -> p (r g b t)"),
+            )
+
+        gates_of = {}
+
+        def plain_rows(r):
+            q, i = divmod(r, PAIR)
+            if i == 0:
+                gates_of[q] = gate_pool.tile([P, PAIR, GATES], F32, name="gates")
+            gates = gates_of[q][:, i, :]
+            acts_t = acts_t_of[r]
+            for c0, n in CHUNKS:
+                bias_in_psum = c0 >= BIAS_IN_PSUM_FROM
+                acc = psum.tile([P, BANK], F32, name="acc_plain", tag="bank")
+                for g0, width, s in PLAIN_GROUPS:
+                    if c0 <= g0 < c0 + n:
+                        cols = acc[:, g0 - c0 : g0 - c0 + width]
+                        for kt in range(KT):
+                            nc.tensor.matmul(
+                                cols,
+                                lhsT=acts_t[:, s, kt, :],
+                                rhs=wplain_t[:, kt, g0 : g0 + width],
+                                start=(kt == 0),
+                                stop=(kt == KT - 1 and not bias_in_psum),
+                            )
+                        if bias_in_psum:
+                            nc.tensor.matmul(
+                                cols, lhsT=ones[:], rhs=bias_rows[:, g0 : g0 + width], start=False, stop=True
+                            )
+                if bias_in_psum:
+                    nc.scalar.copy(out=gates[:, c0 : c0 + n], in_=acc[:, 0:n])
+                else:
+                    nc.vector.tensor_tensor(
+                        out=gates[:, c0 : c0 + n], in0=acc[:, 0:n], in1=bias_bc[:, c0 : c0 + n], op=ALU.add
+                    )
+
+        def mx_rows(r, chunk_ids):
+            gates = gates_of[r // PAIR][:, r % PAIR, :]
+            for j in chunk_ids:
+                c0, n = CHUNKS[j]
+                acc = psum.tile([P, BANK], F32, name="acc_mx", tag="bank")
+                for g in range(PASSES):
+                    nc.tensor.matmul_mx(
+                        out=acc[:, 0:n],
+                        lhsT=x_codes[:, r, g, :].bitcast(FP8X4),
+                        lhsT_scale=x_scales[:, r, g, :],
+                        rhs=w_codes[j][:, g, :].bitcast(FP8X4),
+                        rhs_scale=w_scales[j][:, g, :],
+                        start=(g == 0),
+                        stop=(g == PASSES - 1),
+                    )
+                nc.vector.tensor_tensor(
+                    out=gates[:, c0 : c0 + n], in0=acc[:, 0:n], in1=gates[:, c0 : c0 + n], op=ALU.add
+                )
+
+        def squash(q, lo, hi, func):
+            gates = gates_of[q]
+            nc.scalar.activation(out=gates[:, :, lo:hi], in_=gates[:, :, lo:hi], func=func)
+
+        def squash_core(q):
+            squash(q, 0, 3 * DH, ACT.Sigmoid)
+            squash(q, 3 * DH, 4 * DH, ACT.Tanh)
+
+        def squash_shared(q):
+            squash(q, 4 * DH, 7 * DH, ACT.Sigmoid)
+
+        cell_of = {}
+        outs_of = {}
+        t_cell_of = {}
+
+        def gate_views(q):
+            gates = gates_of[q]
+            i_g, f_g, o_g, c_hat = [gates[:, :, k * DH : (k + 1) * DH] for k in range(4)]
+            b_all = gates[:, :, 4 * DH : 7 * DH].rearrange("p i (j d) -> p i j d", j=3)
+            return i_g, f_g, o_g, c_hat, b_all
+
+        def combine_core(q, engine):
+            i_g, f_g, o_g, c_hat, b_all = gate_views(q)
+            cell = work.tile([P, PAIR, DH], F32, name="cell")
+            fresh = work.tile([P, PAIR, DH], F32, name="fresh")
+            cell_of[q] = cell
+            engine.tensor_tensor(out=cell[:], in0=f_g, in1=c_sb[:, rows_of(q), :], op=ALU.mult)
+            engine.tensor_tensor(out=fresh[:], in0=i_g, in1=c_hat, op=ALU.mult)
+            engine.tensor_tensor(out=cell[:], in0=cell[:], in1=fresh[:], op=ALU.add)
+
+        def combine_shared(q, engine):
+            i_g, f_g, o_g, c_hat, b_all = gate_views(q)
+            engine.tensor_tensor(
+                out=b_all, in0=b_all, in1=o_g.unsqueeze(2).to_broadcast([P, PAIR, 3, DH]), op=ALU.subtract
+            )
+
+        def mask_cell(q):
+            cell = cell_of[q]
+            outs = work.tile([P, 5, PAIR, DH], F32, name="outs")
+            t_cell = work.tile([P, PAIR, DH], F32, name="t_cell")
+            outs_of[q] = outs
+            t_cell_of[q] = t_cell
+            row_mask = [mask_f[:, q * PAIR + i : q * PAIR + i + 1] for i in range(PAIR)]
+            for i in range(PAIR):
+                nc.scalar.activation(out=t_cell[:, i, :], in_=cell[:, i, :], func=ACT.Tanh, scale=row_mask[i])
+            for i in range(PAIR):
+                nc.scalar.activation(out=t_cell[:, i, :], in_=t_cell[:, i, :], func=ACT.Copy, scale=row_mask[i])
+            for i in range(PAIR):
+                nc.scalar.activation(out=outs[:, 1, i, :], in_=cell[:, i, :], func=ACT.Copy, scale=row_mask[i])
+            nc.sync.dma_start(out=out_views[1][:, rows_of(q), :], in_=outs[:, 1, :, :])
+
+        def finish(q):
+            i_g, f_g, o_g, c_hat, b_minus_o = gate_views(q)
+            outs = outs_of[q]
+            t_cell = t_cell_of[q]
+            h_out, c_out, firstout, s1_out, s2_out = [outs[:, k, :, :] for k in range(5)]
+            e1 = work.tile([P, PAIR, DH], F32, name="e1")
+            e2 = work.tile([P, PAIR, DH], F32, name="e2")
+            stt = nc.vector.scalar_tensor_tensor
+            stt(out=firstout, in0=b_minus_o[:, :, 0, :], scalar=1.0, in1=t_cell[:], op0=ALU.add, op1=ALU.mult)
+            nc.vector.tensor_tensor(out=h_out, in0=o_g, in1=t_cell[:], op=ALU.mult)
+            stt(out=e1[:], in0=b_minus_o[:, :, 1, :], scalar=2.0, in1=firstout, op0=ALU.add, op1=ALU.subtract)
+            stt(out=e2[:], in0=firstout, scalar=-2.0, in1=b_minus_o[:, :, 2, :], op0=ALU.mult, op1=ALU.add)
+            stt(out=s1_out, in0=e1[:], scalar=0.5, in1=t_cell[:], op0=ALU.mult, op1=ALU.mult)
+            stt(out=e2[:], in0=e2[:], scalar=3.0, in1=s1_out, op0=ALU.add, op1=ALU.subtract)
+            stt(out=s2_out, in0=e2[:], scalar=1.0 / 3.0, in1=t_cell[:], op0=ALU.mult, op1=ALU.mult)
+            for k in (0, 2, 3, 4):
+                nc.sync.dma_start(out=out_views[k][:, rows_of(q), :], in_=outs[:, k, :, :])
+
+        def helper(q):
+            return nc.vector if q == N_PAIRS - 1 else nc.gpsimd
+
+        def both(stage_of_row_tile, q, *more):
+            for r in range(q * PAIR, (q + 1) * PAIR):
+                stage_of_row_tile(r, *more)
+
+        transpose_plain_weights()
+        broadcast_bias()
+        both(prepare_rows, 0)
+        both(plain_rows, 0)
+        quantise_x(0)
+        regroup_weight_chunk(0)
+        regroup_weight_chunk(1)
+        quantise_weight_chunk(0)
+        quantise_weight_chunk(1)
+        regroup_weight_chunk(2)
+        both(mx_rows, 0, CORE)
+        regroup_weight_chunk(3)
+        both(prepare_rows, 1)
+        squash_core(0)
+        quantise_weight_chunk(2)
+        quantise_weight_chunk(3)
+        combine_core(0, helper(0))
+        nc.vector.tensor_copy(out=mask_f[:], in_=mask_bf[:])
+        quantise_x(1)
+        for q in range(N_PAIRS):
+            if q + 1 < N_PAIRS or N_PAIRS == 1:
+                both(mx_rows, q, SHARED)
+            squash_shared(q)
+            if q + 1 < N_PAIRS:
+                plain_rows((q + 1) * PAIR)
+            mask_cell(q)
+            if q + 1 < N_PAIRS:
+                plain_rows((q + 1) * PAIR + 1)
+                both(mx_rows, q + 1, CORE)
+            if q + 2 < N_PAIRS:
+                both(prepare_rows, q + 2)
+            if q + 2 == N_PAIRS:
+                both(mx_rows, q + 1, SHARED)
+            if q + 1 < N_PAIRS:
+                squash_core(q + 1)
+            combine_shared(q, helper(q))
+            finish(q)
+            if q + 2 < N_PAIRS:
+                quantise_x(q + 2)
+            if q + 1 < N_PAIRS:
+                combine_core(q + 1, helper(q + 1))

@@ -19,15 +19,13 @@ GATES = 7 * DH
 ROW_TILES = BATCH // P
 K_PASS = 4 * P
 PASSES = DI // K_PASS
-KT = DH // P
 BANK = 512
 CHUNKS = ((0, 512), (512, 512), (1024, 512), (1536, 256))
 PLAIN_GROUPS = ((0, 512, 0), (512, 512, 0), (1024, 256, 1), (1280, 256, 2), (1536, 256, 3))
 BIAS_IN_PSUM_FROM = 4 * DH
-PLAIN_ROW_TILES = GATES // P
+W_TILES = GATES // P
 CORE = (0, 1)
 SHARED = (2, 3)
-PER_BANK = 4
 PAIR = 2
 N_PAIRS = ROW_TILES // PAIR
 
@@ -43,9 +41,9 @@ def tile_share_lstm_cell_pa_kernel(
     nc = tc.nc
     with ExitStack() as ctx:
         keep = ctx.enter_context(tc.tile_pool(name="keep", bufs=1))
-        stage = ctx.enter_context(tc.tile_pool(name="stage", bufs=2))
-        gate_pool = ctx.enter_context(tc.tile_pool(name="gate_pool", bufs=3))
-        work = ctx.enter_context(tc.tile_pool(name="work", bufs=2))
+        stage = ctx.enter_context(tc.tile_pool(name="stage", bufs=3))
+        gate_pool = ctx.enter_context(tc.tile_pool(name="gate_pool", bufs=6))
+        work = ctx.enter_context(tc.tile_pool(name="work", bufs=3))
         psum = ctx.enter_context(tc.psum_pool(name="psum", bufs=8))
         ctx.enter_context(tc.manual_schedule())
 
@@ -53,38 +51,33 @@ def tile_share_lstm_cell_pa_kernel(
             return ap.rearrange("(p r) d -> p r d", r=ROW_TILES)
 
         x_view = by_row_tile(x)
+        c_view = by_row_tile(c_minors)
         act_views = [by_row_tile(a) for a in (h_minors, s0, s1, s2)]
         out_views = [by_row_tile(o) for o in (out_0, out_1, out_2, out_3, out_4)]
 
         x_sb = keep.tile([P, ROW_TILES, DI], BF16)
         acts_sb = keep.tile([P, 4, ROW_TILES, DH], BF16)
         c_sb = keep.tile([P, ROW_TILES, DH], BF16)
-        wih_sb = keep.tile([P, GATES // P, DI], BF16)
-        wplain_sb = keep.tile([P, PLAIN_ROW_TILES, DH], BF16)
-        wplain_t = keep.tile([P, KT, GATES], BF16)
+        wih_sb = keep.tile([P, W_TILES, DI], BF16)
+        wplain_sb = keep.tile([P, W_TILES, DH], BF16)
+        wplain_t = keep.tile([P, GATES, 2], BF16)
         bias_rows = keep.tile([P, GATES], BF16)
         bias_bc = keep.tile([P, BIAS_IN_PSUM_FROM], F32)
         mask_bf = keep.tile([P, ROW_TILES], BF16)
         mask_f = keep.tile([P, ROW_TILES], F32)
-        ident_bf = keep.tile([P, P], BF16)
+        cm = keep.tile([P, ROW_TILES, DH], F32)
         ident_f = keep.tile([P, P], F32)
         ones = keep.tile([P, P], BF16)
         warm = keep.tile([P, 1], F32)
         x_codes = keep.tile([P, ROW_TILES, PASSES, P], U32, align_bytes=64)
         x_scales = keep.tile([P, ROW_TILES, PASSES, P], U8, align_bytes=64)
-        w_codes = [
-            keep.tile([P, PASSES, n], U32, align_bytes=64, name="w_codes%d" % j)
-            for j, (c0, n) in enumerate(CHUNKS)
-        ]
-        w_scales = [
-            keep.tile([P, PASSES, n], U8, align_bytes=64, name="w_scales%d" % j)
-            for j, (c0, n) in enumerate(CHUNKS)
-        ]
+        w_codes = keep.tile([P, PASSES, GATES], U32, align_bytes=64)
+        w_scales = keep.tile([P, PASSES, GATES], U8, align_bytes=64)
 
+        nc.vector.memset(bias_rows[:].bitcast(F32), 0.0)
+        make_identity(nc, ident_f[:])
         nc.vector.memset(warm[:], 0.0)
-        nc.vector.memset(bias_rows[:], 0.0)
         nc.vector.memset(ones[:], 1.0)
-        make_identity(nc, ident_bf[:])
 
         def as_row(vec):
             return vec.rearrange("(o n) -> o n", o=1)
@@ -92,63 +85,58 @@ def tile_share_lstm_cell_pa_kernel(
         nc.scalar.dma_start(out=bias_rows[0:1, :], in_=as_row(bias_ih))
         nc.scalar.dma_start(out=bias_rows[1:2, 0 : 4 * DH], in_=as_row(bias_hh))
         for j, b in enumerate((bias_sh0, bias_sh1, bias_sh2)):
-            nc.gpsimd.dma_start(out=bias_rows[1:2, (4 + j) * DH : (5 + j) * DH], in_=as_row(b))
-        nc.gpsimd.dma_start(out=mask_bf[:], in_=mask.rearrange("(p r) -> p r", r=ROW_TILES))
-        make_identity(nc, ident_f[:])
+            nc.scalar.dma_start(out=bias_rows[1:2, (4 + j) * DH : (5 + j) * DH], in_=as_row(b))
         nc.scalar.activation(out=warm[:], in_=warm[:], func=ACT.Sigmoid)
+        nc.gpsimd.dma_start(out=mask_bf[:], in_=mask.rearrange("(p r) -> p r", r=ROW_TILES))
 
-        def load_weight_chunk(j):
-            c0, n = CHUNKS[j]
+        def load_weight_tiles(t0, count):
             nc.sync.dma_start(
-                out=wih_sb[:, c0 // P : (c0 + n) // P, :],
-                in_=weight_ih[c0 : c0 + n, :].rearrange("(t p) k -> p t k", p=P),
+                out=wih_sb[:, t0 : t0 + count, :],
+                in_=weight_ih[t0 * P : (t0 + count) * P, :].rearrange("(t p) k -> p t k", p=P),
             )
 
-        def load_rows(first, count):
-            rows = slice(first, first + count)
-            for s in range(4):
-                nc.sync.dma_start(out=acts_sb[:, s, rows, :], in_=act_views[s][:, rows, :])
-            nc.sync.dma_start(out=x_sb[:, rows, :], in_=x_view[:, rows, :])
+        def load_x(first, count):
+            nc.sync.dma_start(out=x_sb[:, first : first + count, :], in_=x_view[:, first : first + count, :])
 
+        def load_acts(first, count, which=(0, 1, 2, 3)):
+            rows = slice(first, first + count)
+            for s in which:
+                nc.sync.dma_start(out=acts_sb[:, s, rows, :], in_=act_views[s][:, rows, :])
+
+        load_acts(0, 2, (0,))
         nc.sync.dma_start(
             out=wplain_sb[:, 0:8, :], in_=weight_hh.rearrange("(t p) k -> p t k", p=P)
         )
+        load_x(0, 2)
+        for t in range(0, 8, 2):
+            load_weight_tiles(t, 2)
+        nc.sync.dma_start(out=c_sb[:], in_=c_view)
         for j, w in enumerate((weight_sh0, weight_sh1, weight_sh2)):
             nc.sync.dma_start(
                 out=wplain_sb[:, 8 + 2 * j : 10 + 2 * j, :],
                 in_=w.rearrange("(t p) k -> p t k", p=P),
             )
-        load_rows(0, 2)
-        load_weight_chunk(0)
-        load_weight_chunk(1)
-        nc.sync.dma_start(out=c_sb[:], in_=by_row_tile(c_minors))
-        load_weight_chunk(2)
-        load_weight_chunk(3)
-        load_rows(2, 2)
-        load_rows(4, 4)
+        load_acts(0, 2, (1, 2, 3))
+        load_x(2, 2)
+        load_acts(2, 2)
+        for t in range(8, 14, 2):
+            load_weight_tiles(t, 2)
+        load_x(4, 4)
+        load_acts(4, 4)
 
-        def copy_out(turn, out, in_):
-            if turn % 2 == 0:
+        def copy_out(engine, out, in_):
+            if engine == "S":
                 nc.scalar.copy(out=out, in_=in_)
             else:
                 nc.vector.tensor_copy(out=out, in_=in_)
 
-        def transpose_plain_weights():
-            turn = 0
-            for t0 in range(0, PLAIN_ROW_TILES, PER_BANK):
-                count = min(PER_BANK, PLAIN_ROW_TILES - t0)
-                for kt in range(KT):
-                    bank = psum.tile([P, PER_BANK, P], BF16, name="bank_w", tag="bank")
-                    for t in range(count):
-                        nc.tensor.transpose(
-                            bank[:, t, :], wplain_sb[:, t0 + t, kt * P : (kt + 1) * P], ident_bf[:]
-                        )
-                    copy_out(
-                        turn,
-                        wplain_t[:, kt, t0 * P : (t0 + count) * P],
-                        bank[:, 0:count, :].rearrange("p t n -> p (t n)"),
-                    )
-                    turn += 1
+        def plain_weights(t0, count, engine):
+            bank = psum.tile([P, 4, P], F32, name="bank_w", tag="bank")
+            words = wplain_sb[:].bitcast(F32)
+            for t in range(count):
+                nc.tensor.transpose(bank[:, t, :], words[:, t0 + t, :], ident_f[:])
+            out = wplain_t[:].rearrange("p n e -> p (n e)").bitcast(F32)
+            copy_out(engine, out[:, t0 * P : (t0 + count) * P], bank[:, 0:count, :].rearrange("p t n -> p (t n)"))
 
         def broadcast_bias():
             for c0, n in CHUNKS:
@@ -159,231 +147,276 @@ def tile_share_lstm_cell_pa_kernel(
                     )
                     nc.vector.tensor_copy(out=bias_bc[:, c0 : c0 + n], in_=acc[:, 0:n])
 
-        def regroup(turn, rows_bf16, grouped_words):
+        def regroup(engine, rows_bf16, grouped_words):
             words = rows_bf16.bitcast(F32)
-            bank = psum.tile([P, 2 * PASSES, P], F32, name="bank_q", tag="bank")
+            bank = psum.tile([P, PASSES, 2, P], F32, name="bank_q", tag="bank")
             for g in range(PASSES):
                 for u in range(2):
                     nc.tensor.transpose(
-                        bank[:, 2 * g + u, :], words[:, 2 * P * g + u : 2 * P * (g + 1) : 2], ident_f[:]
+                        bank[:, g, u, :], words[:, 2 * P * g + u : 2 * P * (g + 1) : 2], ident_f[:]
                     )
-            copy_out(turn, grouped_words, bank[:].rearrange("p (g u) n -> p g n u", u=2))
+            copy_out(engine, grouped_words, bank[:].rearrange("p g u n -> p g n u"))
 
         w_grouped_of = {}
 
-        def regroup_weight_chunk(j):
-            c0, n = CHUNKS[j]
-            grouped = stage.tile(
-                [P, PASSES, n, 4], BF16, align_bytes=64, name="w_grouped", tag="w_grouped"
-            )
-            w_grouped_of[j] = grouped
-            grouped_words = grouped[:].bitcast(F32)
-            for t in range(n // P):
-                regroup(t, wih_sb[:, c0 // P + t, :], grouped_words[:, :, t * P : (t + 1) * P, :])
+        def weight_tile(t, engine):
+            q, i = divmod(t, 2)
+            if i == 0:
+                w_grouped_of[q] = stage.tile([P, PASSES, 2 * P, 4], BF16, align_bytes=64, name="w_grouped")
+            words = w_grouped_of[q][:].bitcast(F32)
+            regroup(engine, wih_sb[:, t, :], words[:, :, i * P : (i + 1) * P, :])
 
-        def quantise_weight_chunk(j):
-            nc.vector.quantize_mx(
-                out=w_codes[j][:].rearrange("p g n -> p (g n)").bitcast(FP8X4),
-                scales=w_scales[j][:].rearrange("p g n -> p (g n)"),
-                in_=w_grouped_of[j][:].rearrange("p g n t -> p (g n t)"),
-            )
+        def quantise_weights(q):
+            cols = slice(2 * P * q, 2 * P * (q + 1))
+            for g in range(PASSES):
+                nc.vector.quantize_mx(
+                    out=w_codes[:, g, cols].bitcast(FP8X4),
+                    scales=w_scales[:, g, cols],
+                    in_=w_grouped_of[q][:, g, :, :].rearrange("p n t -> p (n t)"),
+                )
 
         x_grouped_of = {}
         acts_t_of = {}
 
-        def prepare_rows(r):
-            acts_t_of[r] = stage.tile([P, 4, KT, P], BF16, name="acts_t", bufs=2 * PAIR)
-            for first in range(0, 4, PER_BANK // KT):
-                bank = psum.tile([P, PER_BANK // KT, KT, P], BF16, name="bank_a", tag="bank")
-                for s in range(PER_BANK // KT):
-                    for kt in range(KT):
-                        nc.tensor.transpose(
-                            bank[:, s, kt, :], acts_sb[:, first + s, r, kt * P : (kt + 1) * P], ident_bf[:]
-                        )
-                nc.scalar.copy(out=acts_t_of[r][:, first : first + PER_BANK // KT, :, :], in_=bank[:])
-            q, i = divmod(r, PAIR)
-            if i == 0:
-                x_grouped_of[q] = stage.tile(
-                    [P, PAIR, PASSES, P, 4], BF16, align_bytes=64, name="x_grouped"
-                )
-            regroup(0, x_sb[:, r, :], x_grouped_of[q][:].bitcast(F32)[:, i, :, :, :])
+        def prepare_x(r, engine):
+            x_grouped_of[r] = stage.tile([P, PASSES, P, 4], BF16, align_bytes=64, name="x_grouped")
+            regroup(engine, x_sb[:, r, :], x_grouped_of[r][:].bitcast(F32))
 
-        def rows_of(q):
-            return slice(q * PAIR, (q + 1) * PAIR)
-
-        def quantise_x(q):
+        def quantise_x(r):
             nc.vector.quantize_mx(
-                out=x_codes[:, rows_of(q), :, :].rearrange("p r g b -> p (r g b)").bitcast(FP8X4),
-                scales=x_scales[:, rows_of(q), :, :].rearrange("p r g b -> p (r g b)"),
-                in_=x_grouped_of[q][:].rearrange("p r g b t -> p (r g b t)"),
+                out=x_codes[:, r, :, :].rearrange("p g b -> p (g b)").bitcast(FP8X4),
+                scales=x_scales[:, r, :, :].rearrange("p g b -> p (g b)"),
+                in_=x_grouped_of[r][:].rearrange("p g b t -> p (g b t)"),
             )
+
+        def prepare_acts(r, which, engine):
+            if r not in acts_t_of:
+                acts_t_of[r] = stage.tile([P, 4, P, 2], BF16, name="acts_t", bufs=4)
+            words = acts_sb[:].bitcast(F32)
+            bank = psum.tile([P, 4, P], F32, name="bank_a", tag="bank")
+            for j, s in enumerate(which):
+                nc.tensor.transpose(bank[:, j, :], words[:, s, r, :], ident_f[:])
+            out = acts_t_of[r][:].rearrange("p s b e -> p s (b e)").bitcast(F32)
+            copy_out(engine, out[:, which[0] : which[-1] + 1, :], bank[:, 0 : len(which), :])
 
         gates_of = {}
 
-        def plain_rows(r):
-            q, i = divmod(r, PAIR)
-            if i == 0:
-                gates_of[q] = gate_pool.tile([P, PAIR, GATES], F32, name="gates")
-            gates = gates_of[q][:, i, :]
-            acts_t = acts_t_of[r]
-            for c0, n in CHUNKS:
-                bias_in_psum = c0 >= BIAS_IN_PSUM_FROM
-                acc = psum.tile([P, BANK], F32, name="acc_plain", tag="bank")
-                for g0, width, s in PLAIN_GROUPS:
-                    if c0 <= g0 < c0 + n:
-                        cols = acc[:, g0 - c0 : g0 - c0 + width]
-                        for kt in range(KT):
-                            nc.tensor.matmul(
-                                cols,
-                                lhsT=acts_t[:, s, kt, :],
-                                rhs=wplain_t[:, kt, g0 : g0 + width],
-                                start=(kt == 0),
-                                stop=(kt == KT - 1 and not bias_in_psum),
-                            )
-                        if bias_in_psum:
-                            nc.tensor.matmul(
-                                cols, lhsT=ones[:], rhs=bias_rows[:, g0 : g0 + width], start=False, stop=True
-                            )
-                if bias_in_psum:
-                    nc.scalar.copy(out=gates[:, c0 : c0 + n], in_=acc[:, 0:n])
-                else:
-                    nc.vector.tensor_tensor(
-                        out=gates[:, c0 : c0 + n], in0=acc[:, 0:n], in1=bias_bc[:, c0 : c0 + n], op=ALU.add
-                    )
+        def plain(r, j, engine):
+            if r not in gates_of:
+                gates_of[r] = gate_pool.tile([P, GATES], F32, name="gates")
+            c0, n = CHUNKS[j]
+            gates = gates_of[r][:, c0 : c0 + n]
+            bias_in_psum = engine == "S"
+            acc = psum.tile([P, BANK], F32, name="acc_plain", tag="bank")
+            for g0, width, s in PLAIN_GROUPS:
+                if c0 <= g0 < c0 + n:
+                    cols = acc[:, g0 - c0 : g0 - c0 + width]
+                    for e in range(2):
+                        nc.tensor.matmul(
+                            cols,
+                            lhsT=acts_t_of[r][:, s, :, e],
+                            rhs=wplain_t[:, g0 : g0 + width, e],
+                            start=(e == 0),
+                            stop=(e == 1 and not bias_in_psum),
+                        )
+                    if bias_in_psum:
+                        nc.tensor.matmul(
+                            cols, lhsT=ones[:], rhs=bias_rows[:, g0 : g0 + width], start=False, stop=True
+                        )
+            if bias_in_psum:
+                nc.scalar.copy(out=gates, in_=acc[:, 0:n])
+            else:
+                nc.vector.tensor_tensor(out=gates, in0=acc[:, 0:n], in1=bias_bc[:, c0 : c0 + n], op=ALU.add)
 
-        def mx_rows(r, chunk_ids):
-            gates = gates_of[r // PAIR][:, r % PAIR, :]
-            for j in chunk_ids:
-                c0, n = CHUNKS[j]
-                acc = psum.tile([P, BANK], F32, name="acc_mx", tag="bank")
-                for g in range(PASSES):
-                    nc.tensor.matmul_mx(
-                        out=acc[:, 0:n],
-                        lhsT=x_codes[:, r, g, :].bitcast(FP8X4),
-                        lhsT_scale=x_scales[:, r, g, :],
-                        rhs=w_codes[j][:, g, :].bitcast(FP8X4),
-                        rhs_scale=w_scales[j][:, g, :],
-                        start=(g == 0),
-                        stop=(g == PASSES - 1),
-                    )
-                nc.vector.tensor_tensor(
-                    out=gates[:, c0 : c0 + n], in0=acc[:, 0:n], in1=gates[:, c0 : c0 + n], op=ALU.add
+        acc_of = {}
+
+        def mx(r, j):
+            c0, n = CHUNKS[j]
+            acc = psum.tile([P, BANK], F32, name="acc_mx", tag="bank")
+            acc_of[r, j] = acc
+            for g in range(PASSES):
+                nc.tensor.matmul_mx(
+                    out=acc[:, 0:n],
+                    lhsT=x_codes[:, r, g, :].bitcast(FP8X4),
+                    lhsT_scale=x_scales[:, r, g, :],
+                    rhs=w_codes[:, g, c0 : c0 + n].bitcast(FP8X4),
+                    rhs_scale=w_scales[:, g, c0 : c0 + n],
+                    start=(g == 0),
+                    stop=(g == PASSES - 1),
                 )
 
-        def squash(q, lo, hi, func):
-            gates = gates_of[q]
-            nc.scalar.activation(out=gates[:, :, lo:hi], in_=gates[:, :, lo:hi], func=func)
+        def add_mx(r, j):
+            c0, n = CHUNKS[j]
+            gates = gates_of[r][:, c0 : c0 + n]
+            nc.vector.tensor_tensor(out=gates, in0=acc_of[r, j][:, 0:n], in1=gates, op=ALU.add)
 
-        def squash_core(q):
-            squash(q, 0, 3 * DH, ACT.Sigmoid)
-            squash(q, 3 * DH, 4 * DH, ACT.Tanh)
+        def squash(r, lo, hi, func):
+            gates = gates_of[r][:, lo:hi]
+            nc.scalar.activation(out=gates, in_=gates, func=func)
 
-        def squash_shared(q):
-            squash(q, 4 * DH, 7 * DH, ACT.Sigmoid)
+        def squash_core(r):
+            squash(r, 0, 3 * DH, ACT.Sigmoid)
+            squash(r, 3 * DH, 4 * DH, ACT.Tanh)
 
-        cell_of = {}
+        def squash_shared(r):
+            squash(r, 4 * DH, 7 * DH, ACT.Sigmoid)
+
+        fc_of = {}
+        fresh_of = {}
         outs_of = {}
         t_cell_of = {}
 
-        def gate_views(q):
-            gates = gates_of[q]
-            i_g, f_g, o_g, c_hat = [gates[:, :, k * DH : (k + 1) * DH] for k in range(4)]
-            b_all = gates[:, :, 4 * DH : 7 * DH].rearrange("p i (j d) -> p i j d", j=3)
-            return i_g, f_g, o_g, c_hat, b_all
+        def gate(r, k):
+            return gates_of[r][:, k * DH : (k + 1) * DH]
 
-        def combine_core(q, engine):
-            i_g, f_g, o_g, c_hat, b_all = gate_views(q)
-            cell = work.tile([P, PAIR, DH], F32, name="cell")
-            fresh = work.tile([P, PAIR, DH], F32, name="fresh")
-            cell_of[q] = cell
-            engine.tensor_tensor(out=cell[:], in0=f_g, in1=c_sb[:, rows_of(q), :], op=ALU.mult)
-            engine.tensor_tensor(out=fresh[:], in0=i_g, in1=c_hat, op=ALU.mult)
-            engine.tensor_tensor(out=cell[:], in0=cell[:], in1=fresh[:], op=ALU.add)
+        def row_mask(r):
+            return mask_f[:, r : r + 1]
 
-        def combine_shared(q, engine):
-            i_g, f_g, o_g, c_hat, b_all = gate_views(q)
-            engine.tensor_tensor(
-                out=b_all, in0=b_all, in1=o_g.unsqueeze(2).to_broadcast([P, PAIR, 3, DH]), op=ALU.subtract
+        def mask_c(r):
+            nc.gpsimd.tensor_scalar(
+                out=cm[:, r, :], in0=c_sb[:, r, :], scalar1=row_mask(r), scalar2=0.0, op0=ALU.mult, op1=ALU.add
             )
 
-        def mask_cell(q):
-            cell = cell_of[q]
-            outs = work.tile([P, 5, PAIR, DH], F32, name="outs")
-            t_cell = work.tile([P, PAIR, DH], F32, name="t_cell")
-            outs_of[q] = outs
-            t_cell_of[q] = t_cell
-            row_mask = [mask_f[:, q * PAIR + i : q * PAIR + i + 1] for i in range(PAIR)]
-            for i in range(PAIR):
-                nc.scalar.activation(out=t_cell[:, i, :], in_=cell[:, i, :], func=ACT.Tanh, scale=row_mask[i])
-            for i in range(PAIR):
-                nc.scalar.activation(out=t_cell[:, i, :], in_=t_cell[:, i, :], func=ACT.Copy, scale=row_mask[i])
-            for i in range(PAIR):
-                nc.scalar.activation(out=outs[:, 1, i, :], in_=cell[:, i, :], func=ACT.Copy, scale=row_mask[i])
-            nc.sync.dma_start(out=out_views[1][:, rows_of(q), :], in_=outs[:, 1, :, :])
+        def products(r, engine):
+            fc_of[r] = work.tile([P, DH], F32, name="fc")
+            fresh_of[r] = work.tile([P, DH], F32, name="fresh")
+            engine.tensor_tensor(out=fc_of[r][:], in0=gate(r, 1), in1=cm[:, r, :], op=ALU.mult)
+            engine.tensor_tensor(out=fresh_of[r][:], in0=gate(r, 0), in1=gate(r, 3), op=ALU.mult)
 
-        def finish(q):
-            i_g, f_g, o_g, c_hat, b_minus_o = gate_views(q)
-            outs = outs_of[q]
-            t_cell = t_cell_of[q]
-            h_out, c_out, firstout, s1_out, s2_out = [outs[:, k, :, :] for k in range(5)]
-            e1 = work.tile([P, PAIR, DH], F32, name="e1")
-            e2 = work.tile([P, PAIR, DH], F32, name="e2")
+        def store(r, k):
+            nc.sync.dma_start(out=out_views[k][:, r, :], in_=outs_of[r][:, k, :])
+
+        def cell(r):
+            outs_of[r] = work.tile([P, 5, DH], F32, name="outs")
+            nc.vector.scalar_tensor_tensor(
+                out=outs_of[r][:, 1, :], in0=fresh_of[r][:], scalar=row_mask(r),
+                in1=fc_of[r][:], op0=ALU.mult, op1=ALU.add,
+            )
+            store(r, 1)
+
+        def tanh_cell(r):
+            t_cell_of[r] = work.tile([P, DH], F32, name="t_cell")
+            t_cell = t_cell_of[r][:]
+            nc.scalar.activation(out=t_cell, in_=outs_of[r][:, 1, :], func=ACT.Tanh)
+
+        def mask_tanh(r):
+            t_cell = t_cell_of[r][:]
+            nc.scalar.activation(out=t_cell, in_=t_cell, func=ACT.Copy, scale=row_mask(r))
+
+        def hidden(r, engine):
+            engine.tensor_tensor(out=outs_of[r][:, 0, :], in0=gate(r, 2), in1=t_cell_of[r][:], op=ALU.mult)
+            store(r, 0)
+
+        def minus_o(r, engine):
+            b_all = gates_of[r][:, 4 * DH : 7 * DH].rearrange("p (j d) -> p j d", j=3)
+            engine.tensor_tensor(
+                out=b_all, in0=b_all, in1=gate(r, 2).unsqueeze(1).to_broadcast([P, 3, DH]), op=ALU.subtract
+            )
+
+        e_of = {}
+
+        def finish(r, step):
             stt = nc.vector.scalar_tensor_tensor
-            stt(out=firstout, in0=b_minus_o[:, :, 0, :], scalar=1.0, in1=t_cell[:], op0=ALU.add, op1=ALU.mult)
-            nc.vector.tensor_tensor(out=h_out, in0=o_g, in1=t_cell[:], op=ALU.mult)
-            stt(out=e1[:], in0=b_minus_o[:, :, 1, :], scalar=2.0, in1=firstout, op0=ALU.add, op1=ALU.subtract)
-            stt(out=e2[:], in0=firstout, scalar=-2.0, in1=b_minus_o[:, :, 2, :], op0=ALU.mult, op1=ALU.add)
-            stt(out=s1_out, in0=e1[:], scalar=0.5, in1=t_cell[:], op0=ALU.mult, op1=ALU.mult)
-            stt(out=e2[:], in0=e2[:], scalar=3.0, in1=s1_out, op0=ALU.add, op1=ALU.subtract)
-            stt(out=s2_out, in0=e2[:], scalar=1.0 / 3.0, in1=t_cell[:], op0=ALU.mult, op1=ALU.mult)
-            for k in (0, 2, 3, 4):
-                nc.sync.dma_start(out=out_views[k][:, rows_of(q), :], in_=outs[:, k, :, :])
+            t_cell = t_cell_of[r][:]
+            s0_out, s1_out, s2_out = [outs_of[r][:, k, :] for k in (2, 3, 4)]
+            if step == 0:
+                e_of[r] = (work.tile([P, DH], F32, name="e1"), work.tile([P, DH], F32, name="e2"))
+                stt(out=s0_out, in0=gate(r, 4), scalar=1.0, in1=t_cell, op0=ALU.add, op1=ALU.mult)
+                store(r, 2)
+            e1, e2 = e_of[r]
+            if step == 1:
+                stt(out=e1[:], in0=gate(r, 5), scalar=2.0, in1=s0_out, op0=ALU.add, op1=ALU.subtract)
+                stt(out=e2[:], in0=s0_out, scalar=-2.0, in1=gate(r, 6), op0=ALU.mult, op1=ALU.add)
+            if step == 2:
+                stt(out=s1_out, in0=e1[:], scalar=0.5, in1=t_cell, op0=ALU.mult, op1=ALU.mult)
+                store(r, 3)
+            if step == 3:
+                stt(out=e2[:], in0=e2[:], scalar=3.0, in1=s1_out, op0=ALU.add, op1=ALU.subtract)
+            if step == 4:
+                stt(out=s2_out, in0=e2[:], scalar=1.0 / 3.0, in1=t_cell, op0=ALU.mult, op1=ALU.mult)
+                store(r, 4)
 
-        def helper(q):
-            return nc.vector if q == N_PAIRS - 1 else nc.gpsimd
+        G = nc.gpsimd
+        V = nc.vector
 
-        def both(stage_of_row_tile, q, *more):
-            for r in range(q * PAIR, (q + 1) * PAIR):
-                stage_of_row_tile(r, *more)
-
-        transpose_plain_weights()
-        broadcast_bias()
-        both(prepare_rows, 0)
-        both(plain_rows, 0)
+        prepare_acts(0, (0,), "S")
+        plain_weights(0, 4, "V")
+        plain_weights(4, 4, "S")
+        prepare_x(0, "V")
         quantise_x(0)
-        regroup_weight_chunk(0)
-        regroup_weight_chunk(1)
-        quantise_weight_chunk(0)
-        quantise_weight_chunk(1)
-        regroup_weight_chunk(2)
-        both(mx_rows, 0, CORE)
-        regroup_weight_chunk(3)
-        both(prepare_rows, 1)
-        squash_core(0)
-        quantise_weight_chunk(2)
-        quantise_weight_chunk(3)
-        combine_core(0, helper(0))
+        for t in range(4):
+            weight_tile(t, "SVSSSVSS"[t])
+            if t % 2 == 1:
+                quantise_weights(t // 2)
+        broadcast_bias()
+        plain(0, 0, "V")
+        plain(0, 1, "V")
+        mx(0, 0)
         nc.vector.tensor_copy(out=mask_f[:], in_=mask_bf[:])
-        quantise_x(1)
-        for q in range(N_PAIRS):
-            if q + 1 < N_PAIRS or N_PAIRS == 1:
-                both(mx_rows, q, SHARED)
-            squash_shared(q)
-            if q + 1 < N_PAIRS:
-                plain_rows((q + 1) * PAIR)
-            mask_cell(q)
-            if q + 1 < N_PAIRS:
-                plain_rows((q + 1) * PAIR + 1)
-                both(mx_rows, q + 1, CORE)
-            if q + 2 < N_PAIRS:
-                both(prepare_rows, q + 2)
-            if q + 2 == N_PAIRS:
-                both(mx_rows, q + 1, SHARED)
-            if q + 1 < N_PAIRS:
-                squash_core(q + 1)
-            combine_shared(q, helper(q))
-            finish(q)
-            if q + 2 < N_PAIRS:
-                quantise_x(q + 2)
-            if q + 1 < N_PAIRS:
-                combine_core(q + 1, helper(q + 1))
+        for r in range(ROW_TILES):
+            mask_c(r)
+        for t in range(4, 8):
+            weight_tile(t, "SVSSSVSS"[t])
+            if t % 2 == 1:
+                quantise_weights(t // 2)
+            if t == 5:
+                add_mx(0, 0)
+        prepare_acts(0, (1, 2, 3), "S")
+        plain_weights(8, 4, "S")
+        plain_weights(12, 2, "S")
+        def live(r):
+            return 0 <= r < ROW_TILES
+
+        for n in range(ROW_TILES + 3):
+            last = n >= ROW_TILES
+            if live(n + 1):
+                prepare_acts(n + 1, (0,), "S")
+                prepare_x(n + 1, "S")
+            if live(n) and n > 0:
+                plain(n, 0, "V")
+            if live(n - 1):
+                cell(n - 1)
+                tanh_cell(n - 1)
+            if live(n) and n > 0:
+                plain(n, 1, "V")
+            if live(n - 1):
+                mask_tanh(n - 1)
+                hidden(n - 1, G)
+            if live(n - 3):
+                finish(n - 3, 3)
+            if live(n + 1):
+                quantise_x(n + 1)
+            if live(n - 3):
+                finish(n - 3, 4)
+            if live(n):
+                if n > 0:
+                    mx(n, 0)
+                mx(n, 1)
+                if n > 0:
+                    add_mx(n, 0)
+                add_mx(n, 1)
+            if n == 1:
+                for t in range(8, 14):
+                    weight_tile(t, "SSSSSS"[t - 8])
+                    if t % 2 == 1:
+                        quantise_weights(t // 2)
+            if live(n - 1):
+                plain(n - 1, 2, "S")
+                plain(n - 1, 3, "S")
+            if live(n):
+                squash_core(n)
+                products(n, G)
+            if live(n - 2):
+                finish(n - 2, 0)
+            if live(n - 1):
+                mx(n - 1, 2)
+                mx(n - 1, 3)
+                add_mx(n - 1, 2)
+                add_mx(n - 1, 3)
+                squash_shared(n - 1)
+                minus_o(n - 1, V if last else G)
+            if live(n + 1):
+                prepare_acts(n + 1, (1, 2, 3), "S")
+            if live(n - 2):
+                finish(n - 2, 1)
+                finish(n - 2, 2)

@@ -26,6 +26,7 @@ BIAS_IN_PSUM_FROM = 4 * DH
 W_TILES = GATES // P
 CORE = (0, 1)
 SHARED = (2, 3)
+SLOT = (0, 2, 3, 4, 1)
 PAIR = 2
 N_PAIRS = ROW_TILES // PAIR
 
@@ -65,7 +66,7 @@ def tile_share_lstm_cell_pa_kernel(
         bias_bc = keep.tile([P, BIAS_IN_PSUM_FROM], F32)
         mask_bf = keep.tile([P, ROW_TILES], BF16)
         mask_f = keep.tile([P, ROW_TILES], F32)
-        cm = keep.tile([P, ROW_TILES, DH], F32)
+        mask_third = keep.tile([P, ROW_TILES], F32)
         ident_f = keep.tile([P, P], F32)
         ones = keep.tile([P, P], BF16)
         warm = keep.tile([P, 1], F32)
@@ -201,11 +202,16 @@ def tile_share_lstm_cell_pa_kernel(
 
         gates_of = {}
 
+        def gate_cols(r, lo, hi):
+            shift = 0 if lo < 4 * DH else DH
+            return gates_of[r][:, lo + shift : hi + shift]
+
+
         def plain(r, j, engine):
             if r not in gates_of:
-                gates_of[r] = gate_pool.tile([P, GATES], F32, name="gates")
+                gates_of[r] = gate_pool.tile([P, GATES + DH], F32, name="gates")
             c0, n = CHUNKS[j]
-            gates = gates_of[r][:, c0 : c0 + n]
+            gates = gate_cols(r, c0, c0 + n)
             bias_in_psum = engine == "S"
             acc = psum.tile([P, BANK], F32, name="acc_plain", tag="bank")
             for g0, width, s in PLAIN_GROUPS:
@@ -247,11 +253,11 @@ def tile_share_lstm_cell_pa_kernel(
 
         def add_mx(r, j):
             c0, n = CHUNKS[j]
-            gates = gates_of[r][:, c0 : c0 + n]
+            gates = gate_cols(r, c0, c0 + n)
             nc.vector.tensor_tensor(out=gates, in0=acc_of[r, j][:, 0:n], in1=gates, op=ALU.add)
 
         def squash(r, lo, hi, func):
-            gates = gates_of[r][:, lo:hi]
+            gates = gate_cols(r, lo, hi)
             nc.scalar.activation(out=gates, in_=gates, func=func)
 
         def squash_core(r):
@@ -261,80 +267,97 @@ def tile_share_lstm_cell_pa_kernel(
         def squash_shared(r):
             squash(r, 4 * DH, 7 * DH, ACT.Sigmoid)
 
-        fc_of = {}
-        fresh_of = {}
+        prod_of = {}
         outs_of = {}
         t_cell_of = {}
 
         def gate(r, k):
-            return gates_of[r][:, k * DH : (k + 1) * DH]
+            return gate_cols(r, k * DH, (k + 1) * DH)
 
         def row_mask(r):
             return mask_f[:, r : r + 1]
 
         def mask_c(r):
-            nc.gpsimd.tensor_scalar(
-                out=cm[:, r, :], in0=c_sb[:, r, :], scalar1=row_mask(r), scalar2=0.0, op0=ALU.mult, op1=ALU.add
+            nc.scalar.activation(
+                out=gates_of[r][:, 4 * DH : 5 * DH], in_=c_sb[:, r, :], func=ACT.Copy, scale=row_mask(r)
             )
 
         def products(r, engine):
-            fc_of[r] = work.tile([P, DH], F32, name="fc")
-            fresh_of[r] = work.tile([P, DH], F32, name="fresh")
-            engine.tensor_tensor(out=fc_of[r][:], in0=gate(r, 1), in1=cm[:, r, :], op=ALU.mult)
-            engine.tensor_tensor(out=fresh_of[r][:], in0=gate(r, 0), in1=gate(r, 3), op=ALU.mult)
+            prod_of[r] = work.tile([P, 2 * DH], F32, name="prod")
+            engine.tensor_tensor(
+                out=prod_of[r][:], in0=gates_of[r][:, 0 : 2 * DH], in1=gates_of[r][:, 3 * DH : 5 * DH], op=ALU.mult
+            )
 
         def store(r, k):
-            nc.sync.dma_start(out=out_views[k][:, r, :], in_=outs_of[r][:, k, :])
+            nc.sync.dma_start(out=out_views[k][:, r, :], in_=outs_of[r][:, SLOT[k], :])
 
         def cell(r):
             outs_of[r] = work.tile([P, 5, DH], F32, name="outs")
             nc.vector.scalar_tensor_tensor(
-                out=outs_of[r][:, 1, :], in0=fresh_of[r][:], scalar=row_mask(r),
-                in1=fc_of[r][:], op0=ALU.mult, op1=ALU.add,
+                out=outs_of[r][:, SLOT[1], :], in0=prod_of[r][:, 0:DH], scalar=row_mask(r),
+                in1=prod_of[r][:, DH : 2 * DH], op0=ALU.mult, op1=ALU.add,
             )
             store(r, 1)
 
         def tanh_cell(r):
-            t_cell_of[r] = work.tile([P, DH], F32, name="t_cell")
-            t_cell = t_cell_of[r][:]
-            nc.scalar.activation(out=t_cell, in_=outs_of[r][:, 1, :], func=ACT.Tanh)
+            t_cell_of[r] = work.tile([P, 2, DH], F32, name="t_cell")
+            nc.scalar.activation(out=t_cell_of[r][:, 1, :], in_=outs_of[r][:, SLOT[1], :], func=ACT.Tanh)
 
         def mask_tanh(r):
-            t_cell = t_cell_of[r][:]
-            nc.scalar.activation(out=t_cell, in_=t_cell, func=ACT.Copy, scale=row_mask(r))
+            nc.scalar.activation(
+                out=t_cell_of[r][:, 0, :], in_=t_cell_of[r][:, 1, :], func=ACT.Copy, scale=row_mask(r)
+            )
 
-        def hidden(r, engine):
-            engine.tensor_tensor(out=outs_of[r][:, 0, :], in0=gate(r, 2), in1=t_cell_of[r][:], op=ALU.mult)
-            store(r, 0)
+        def third_tanh(r):
+            third = t_cell_of[r][:, 1, :]
+            nc.scalar.activation(out=third, in_=third, func=ACT.Copy, scale=mask_third[:, r : r + 1])
 
-        def minus_o(r, engine):
-            b_all = gates_of[r][:, 4 * DH : 7 * DH].rearrange("p (j d) -> p j d", j=3)
+        def minus_o(r, first, count, engine):
+            b = gate_cols(r, (4 + first) * DH, (4 + first + count) * DH).rearrange("p (j d) -> p j d", j=count)
             engine.tensor_tensor(
-                out=b_all, in0=b_all, in1=gate(r, 2).unsqueeze(1).to_broadcast([P, 3, DH]), op=ALU.subtract
+                out=b, in0=b, in1=gate(r, 2).unsqueeze(1).to_broadcast([P, count, DH]), op=ALU.subtract
             )
 
         e_of = {}
 
-        def finish(r, step):
+        def finish(r, *steps):
             stt = nc.vector.scalar_tensor_tensor
-            t_cell = t_cell_of[r][:]
-            s0_out, s1_out, s2_out = [outs_of[r][:, k, :] for k in (2, 3, 4)]
-            if step == 0:
-                e_of[r] = (work.tile([P, DH], F32, name="e1"), work.tile([P, DH], F32, name="e2"))
-                stt(out=s0_out, in0=gate(r, 4), scalar=1.0, in1=t_cell, op0=ALU.add, op1=ALU.mult)
-                store(r, 2)
-            e1, e2 = e_of[r]
-            if step == 1:
-                stt(out=e1[:], in0=gate(r, 5), scalar=2.0, in1=s0_out, op0=ALU.add, op1=ALU.subtract)
-                stt(out=e2[:], in0=s0_out, scalar=-2.0, in1=gate(r, 6), op0=ALU.mult, op1=ALU.add)
-            if step == 2:
-                stt(out=s1_out, in0=e1[:], scalar=0.5, in1=t_cell, op0=ALU.mult, op1=ALU.mult)
-                store(r, 3)
-            if step == 3:
-                stt(out=e2[:], in0=e2[:], scalar=3.0, in1=s1_out, op0=ALU.add, op1=ALU.subtract)
-            if step == 4:
-                stt(out=s2_out, in0=e2[:], scalar=1.0 / 3.0, in1=t_cell, op0=ALU.mult, op1=ALU.mult)
-                store(r, 4)
+            t_cell = t_cell_of[r][:, 0, :]
+            s0_out, s1_out = [outs_of[r][:, SLOT[k], :] for k in (2, 3)]
+            if r not in e_of:
+                e_of[r] = work.tile([P, DH], F32, name="e1")
+            e1, e2 = e_of[r][:], gate(r, 3)
+            for step in steps:
+                if step == 0:
+                    stt(out=s0_out, in0=gate(r, 4), scalar=1.0, in1=t_cell, op0=ALU.add, op1=ALU.mult)
+                    store(r, 2)
+                if step == 1:
+                    stt(out=e1, in0=gate(r, 5), scalar=2.0, in1=s0_out, op0=ALU.add, op1=ALU.subtract)
+                if step == 2:
+                    stt(out=e2, in0=s0_out, scalar=-2.0, in1=gate(r, 6), op0=ALU.mult, op1=ALU.add)
+                if step == 3:
+                    stt(out=s1_out, in0=e1, scalar=0.5, in1=t_cell, op0=ALU.mult, op1=ALU.mult)
+                    store(r, 3)
+                if step == 4:
+                    stt(out=e2, in0=e2, scalar=3.0, in1=s1_out, op0=ALU.add, op1=ALU.subtract)
+
+        def first_and_last(r, engine):
+            engine.tensor_tensor(
+                out=outs_of[r][:, 0:2, :],
+                in0=gates_of[r][:, 2 * DH : 4 * DH].rearrange("p (k d) -> p k d", k=2),
+                in1=t_cell_of[r][:],
+                op=ALU.mult,
+            )
+            store(r, 0)
+            store(r, 4)
+
+        def hidden_alone(r, engine):
+            engine.tensor_tensor(out=outs_of[r][:, 0, :], in0=gate(r, 2), in1=t_cell_of[r][:, 0, :], op=ALU.mult)
+            store(r, 0)
+
+        def last_alone(r, engine):
+            engine.tensor_tensor(out=outs_of[r][:, 1, :], in0=gate(r, 3), in1=t_cell_of[r][:, 1, :], op=ALU.mult)
+            store(r, 4)
 
         G = nc.gpsimd
         V = nc.vector
@@ -344,6 +367,7 @@ def tile_share_lstm_cell_pa_kernel(
         plain_weights(4, 4, "S")
         prepare_x(0, "V")
         quantise_x(0)
+        prepare_x(1, "S")
         for t in range(4):
             weight_tile(t, "SVSSSVSS"[t])
             if t % 2 == 1:
@@ -353,41 +377,60 @@ def tile_share_lstm_cell_pa_kernel(
         plain(0, 1, "V")
         mx(0, 0)
         nc.vector.tensor_copy(out=mask_f[:], in_=mask_bf[:])
-        for r in range(ROW_TILES):
-            mask_c(r)
+        nc.vector.tensor_scalar(out=mask_third[:], in0=mask_f[:], scalar1=1.0 / 3.0, scalar2=None, op0=ALU.mult)
         for t in range(4, 8):
             weight_tile(t, "SVSSSVSS"[t])
             if t % 2 == 1:
                 quantise_weights(t // 2)
             if t == 5:
                 add_mx(0, 0)
+                mask_c(0)
+        quantise_x(1)
         prepare_acts(0, (1, 2, 3), "S")
         plain_weights(8, 4, "S")
         plain_weights(12, 2, "S")
+
         def live(r):
             return 0 <= r < ROW_TILES
 
-        for n in range(ROW_TILES + 3):
-            last = n >= ROW_TILES
+        for n in range(ROW_TILES + 4):
             if live(n + 1):
                 prepare_acts(n + 1, (0,), "S")
-                prepare_x(n + 1, "S")
+            if live(n + 2):
+                prepare_x(n + 2, "S")
+            if live(n - 2):
+                tanh_cell(n - 2)
+                mask_tanh(n - 2)
+            if live(n - 3) and n < 9:
+                first_and_last(n - 3, G)
+            if live(n - 1):
+                products(n - 1, G if n < 8 else V)
+            if live(n - 2):
+                if n >= 9 - 1:
+                    hidden_alone(n - 2, G)
+                if n < 9:
+                    minus_o(n - 2, 2, 1, G)
             if live(n) and n > 0:
                 plain(n, 0, "V")
-            if live(n - 1):
-                cell(n - 1)
-                tanh_cell(n - 1)
-            if live(n) and n > 0:
                 plain(n, 1, "V")
+                mask_c(n)
+            if n == 1:
+                for t in (8, 9):
+                    weight_tile(t, "S" if t % 2 == 0 else "V")
+                quantise_weights(4)
+            if n == 1:
+                for t in (10, 11):
+                    weight_tile(t, "S" if t % 2 == 0 else "V")
+                quantise_weights(5)
+            if n == 1:
+                for t in (12, 13):
+                    weight_tile(t, "S" if t % 2 == 0 else "V")
+                quantise_weights(6)
             if live(n - 1):
-                mask_tanh(n - 1)
-                hidden(n - 1, G)
-            if live(n - 3):
-                finish(n - 3, 3)
-            if live(n + 1):
-                quantise_x(n + 1)
-            if live(n - 3):
-                finish(n - 3, 4)
+                plain(n - 1, 2, "S")
+                plain(n - 1, 3, "S")
+            if live(n - 2):
+                third_tanh(n - 2)
             if live(n):
                 if n > 0:
                     mx(n, 0)
@@ -395,28 +438,25 @@ def tile_share_lstm_cell_pa_kernel(
                 if n > 0:
                     add_mx(n, 0)
                 add_mx(n, 1)
-            if n == 1:
-                for t in range(8, 14):
-                    weight_tile(t, "SSSSSS"[t - 8])
-                    if t % 2 == 1:
-                        quantise_weights(t // 2)
-            if live(n - 1):
-                plain(n - 1, 2, "S")
-                plain(n - 1, 3, "S")
-            if live(n):
                 squash_core(n)
-                products(n, G)
-            if live(n - 2):
-                finish(n - 2, 0)
             if live(n - 1):
                 mx(n - 1, 2)
                 mx(n - 1, 3)
                 add_mx(n - 1, 2)
                 add_mx(n - 1, 3)
                 squash_shared(n - 1)
-                minus_o(n - 1, V if last else G)
             if live(n + 1):
                 prepare_acts(n + 1, (1, 2, 3), "S")
             if live(n - 2):
-                finish(n - 2, 1)
-                finish(n - 2, 2)
+                minus_o(n - 2, 0, 2 if n < 9 else 3, V)
+                finish(n - 2, 0)
+            if live(n + 2):
+                quantise_x(n + 2)
+            if live(n - 2):
+                finish(n - 2, 1, 2, 3)
+            if live(n - 1):
+                cell(n - 1)
+            if live(n - 2):
+                finish(n - 2, 4)
+                if n >= 9 - 1:
+                    last_alone(n - 2, V)

@@ -282,9 +282,9 @@ def tile_share_lstm_cell_pa_kernel(
                 out=gates_of[r][:, 4 * DH : 5 * DH], in_=c_sb[:, r, :], func=ACT.Copy, scale=row_mask(r)
             )
 
-        def products(r, engine):
+        def products(r):
             prod_of[r] = work.tile([P, 2 * DH], F32, name="prod")
-            engine.tensor_tensor(
+            nc.vector.tensor_tensor(
                 out=prod_of[r][:], in0=gates_of[r][:, 0 : 2 * DH], in1=gates_of[r][:, 3 * DH : 5 * DH], op=ALU.mult
             )
 
@@ -312,10 +312,10 @@ def tile_share_lstm_cell_pa_kernel(
             third = t_cell_of[r][:, 1, :]
             nc.scalar.activation(out=third, in_=third, func=ACT.Copy, scale=mask_third[:, r : r + 1])
 
-        def minus_o(r, first, count, engine):
-            b = gate_cols(r, (4 + first) * DH, (4 + first + count) * DH).rearrange("p (j d) -> p j d", j=count)
-            engine.tensor_tensor(
-                out=b, in0=b, in1=gate(r, 2).unsqueeze(1).to_broadcast([P, count, DH]), op=ALU.subtract
+        def minus_o(r):
+            b = gate_cols(r, 4 * DH, 7 * DH).rearrange("p (j d) -> p j d", j=3)
+            nc.vector.tensor_tensor(
+                out=b, in0=b, in1=gate(r, 2).unsqueeze(1).to_broadcast([P, 3, DH]), op=ALU.subtract
             )
 
         e_of = {}
@@ -341,8 +341,8 @@ def tile_share_lstm_cell_pa_kernel(
                 if step == 4:
                     stt(out=e2, in0=e2, scalar=3.0, in1=s1_out, op0=ALU.add, op1=ALU.subtract)
 
-        def first_and_last(r, engine):
-            engine.tensor_tensor(
+        def first_and_last(r):
+            nc.vector.tensor_tensor(
                 out=outs_of[r][:, 0:2, :],
                 in0=gates_of[r][:, 2 * DH : 4 * DH].rearrange("p (k d) -> p k d", k=2),
                 in1=t_cell_of[r][:],
@@ -351,16 +351,6 @@ def tile_share_lstm_cell_pa_kernel(
             store(r, 0)
             store(r, 4)
 
-        def hidden_alone(r, engine):
-            engine.tensor_tensor(out=outs_of[r][:, 0, :], in0=gate(r, 2), in1=t_cell_of[r][:, 0, :], op=ALU.mult)
-            store(r, 0)
-
-        def last_alone(r, engine):
-            engine.tensor_tensor(out=outs_of[r][:, 1, :], in0=gate(r, 3), in1=t_cell_of[r][:, 1, :], op=ALU.mult)
-            store(r, 4)
-
-        G = nc.gpsimd
-        V = nc.vector
 
         prepare_acts(0, (0,), "S")
         plain_weights(0, 4, "V")
@@ -401,15 +391,6 @@ def tile_share_lstm_cell_pa_kernel(
             if live(n - 2):
                 tanh_cell(n - 2)
                 mask_tanh(n - 2)
-            if live(n - 3) and n < 9:
-                first_and_last(n - 3, G)
-            if live(n - 1):
-                products(n - 1, G if n < 8 else V)
-            if live(n - 2):
-                if n >= 9 - 1:
-                    hidden_alone(n - 2, G)
-                if n < 9:
-                    minus_o(n - 2, 2, 1, G)
             if live(n) and n > 0:
                 plain(n, 0, "V")
                 plain(n, 1, "V")
@@ -448,7 +429,10 @@ def tile_share_lstm_cell_pa_kernel(
             if live(n + 1):
                 prepare_acts(n + 1, (1, 2, 3), "S")
             if live(n - 2):
-                minus_o(n - 2, 0, 2 if n < 9 else 3, V)
+                minus_o(n - 2)
+            if live(n - 1):
+                products(n - 1)
+            if live(n - 2):
                 finish(n - 2, 0)
             if live(n + 2):
                 quantise_x(n + 2)
@@ -458,5 +442,4 @@ def tile_share_lstm_cell_pa_kernel(
                 cell(n - 1)
             if live(n - 2):
                 finish(n - 2, 4)
-                if n >= 9 - 1:
-                    last_alone(n - 2, V)
+                first_and_last(n - 2)

@@ -17,18 +17,23 @@ DI = 1024
 DH = 256
 GATES = 7 * DH
 ROW_TILES = BATCH // P
+W_TILES = GATES // P
+CORE_TILES = 4 * DH // P
 K_PASS = 4 * P
 PASSES = DI // K_PASS
-BANK = 512
-CHUNKS = ((0, 512), (512, 512), (1024, 512), (1536, 256))
-PLAIN_GROUPS = ((0, 512, 0), (512, 512, 0), (1024, 256, 1), (1280, 256, 2), (1536, 256, 3))
-BIAS_IN_PSUM_FROM = 4 * DH
-W_TILES = GATES // P
-CORE = (0, 1)
-SHARED = (2, 3)
-SLOT = (0, 2, 3, 4, 1)
+ROW_BUFS = 6
+GROUP_BUFS = 3
 PAIR = 2
-N_PAIRS = ROW_TILES // PAIR
+HALF = 512
+HALVES = BATCH // HALF
+TILES_PER_HALF = HALF // P
+PARTS = {
+    "i f": ((0, 2 * DH, 0),),
+    "c_hat": ((3 * DH, DH, 0),),
+    "o b2": ((2 * DH, DH, 0), (6 * DH, DH, 3)),
+    "b0 b1": ((4 * DH, DH, 1), (5 * DH, DH, 2)),
+}
+SLOT = (0, 2, 3, 4, 1)
 
 FLOPS = 2 * BATCH * (GATES * DI + 4 * DH * DH + 3 * DH * DH)
 
@@ -42,9 +47,9 @@ def tile_share_lstm_cell_pa_kernel(
     nc = tc.nc
     with ExitStack() as ctx:
         keep = ctx.enter_context(tc.tile_pool(name="keep", bufs=1))
-        stage = ctx.enter_context(tc.tile_pool(name="stage", bufs=3))
-        gate_pool = ctx.enter_context(tc.tile_pool(name="gate_pool", bufs=6))
-        work = ctx.enter_context(tc.tile_pool(name="work", bufs=3))
+        stage = ctx.enter_context(tc.tile_pool(name="stage", bufs=2))
+        gate_pool = ctx.enter_context(tc.tile_pool(name="gate_pool", bufs=4))
+        work = ctx.enter_context(tc.tile_pool(name="work", bufs=2))
         psum = ctx.enter_context(tc.psum_pool(name="psum", bufs=8))
         ctx.enter_context(tc.manual_schedule())
 
@@ -56,74 +61,81 @@ def tile_share_lstm_cell_pa_kernel(
         act_views = [by_row_tile(a) for a in (h_minors, s0, s1, s2)]
         out_views = [by_row_tile(o) for o in (out_0, out_1, out_2, out_3, out_4)]
 
-        x_sb = keep.tile([P, ROW_TILES, DI], BF16)
         acts_sb = keep.tile([P, 4, ROW_TILES, DH], BF16)
         c_sb = keep.tile([P, ROW_TILES, DH], BF16)
-        wih_sb = keep.tile([P, W_TILES, DI], BF16)
         wplain_sb = keep.tile([P, W_TILES, DH], BF16)
         wplain_t = keep.tile([P, GATES, 2], BF16)
-        bias_rows = keep.tile([P, GATES], BF16)
-        bias_bc = keep.tile([P, BIAS_IN_PSUM_FROM], F32)
+        bias_rows = keep.tile([P, P], BF16)
+        bias_cols = keep.tile([P, 64], F32)
+        bias = keep.tile([P, W_TILES], F32)
         mask_bf = keep.tile([P, ROW_TILES], BF16)
         mask_f = keep.tile([P, ROW_TILES], F32)
         mask_third = keep.tile([P, ROW_TILES], F32)
+        ident_bf = keep.tile([P, P], BF16)
         ident_f = keep.tile([P, P], F32)
-        ones = keep.tile([P, P], BF16)
         warm = keep.tile([P, 1], F32)
-        x_codes = keep.tile([P, ROW_TILES, PASSES, P], U32, align_bytes=64)
-        x_scales = keep.tile([P, ROW_TILES, PASSES, P], U8, align_bytes=64)
+        x_codes = keep.tile([P, HALVES, PASSES, HALF], U32, align_bytes=64)
+        x_scales = keep.tile([P, HALVES, PASSES, HALF], U8, align_bytes=64)
         w_codes = keep.tile([P, PASSES, GATES], U32, align_bytes=64)
         w_scales = keep.tile([P, PASSES, GATES], U8, align_bytes=64)
 
         nc.vector.memset(bias_rows[:].bitcast(F32), 0.0)
-        make_identity(nc, ident_f[:])
         nc.vector.memset(warm[:], 0.0)
-        nc.vector.memset(ones[:], 1.0)
+        make_identity(nc, ident_f[:])
+        make_identity(nc, ident_bf[:])
 
-        def as_row(vec):
-            return vec.rearrange("(o n) -> o n", o=1)
+        def load_bias(first_row, vec):
+            n = vec.shape[0] // P
+            nc.scalar.dma_start(
+                out=bias_rows[first_row : first_row + n, :], in_=vec.rearrange("(t n) -> t n", n=P)
+            )
 
-        nc.scalar.dma_start(out=bias_rows[0:1, :], in_=as_row(bias_ih))
-        nc.scalar.dma_start(out=bias_rows[1:2, 0 : 4 * DH], in_=as_row(bias_hh))
+        load_bias(0, bias_ih)
+        load_bias(32, bias_hh)
         for j, b in enumerate((bias_sh0, bias_sh1, bias_sh2)):
-            nc.scalar.dma_start(out=bias_rows[1:2, (4 + j) * DH : (5 + j) * DH], in_=as_row(b))
+            load_bias(32 + CORE_TILES + 2 * j, b)
         nc.scalar.activation(out=warm[:], in_=warm[:], func=ACT.Sigmoid)
         nc.gpsimd.dma_start(out=mask_bf[:], in_=mask.rearrange("(p r) -> p r", r=ROW_TILES))
 
-        def load_weight_tiles(t0, count):
+        w_rows_of = {}
+        x_rows_of = {}
+
+        def row_pair():
+            return stage.tile([P, PAIR, DI], BF16, name="rows", bufs=ROW_BUFS)
+
+        def load_weight_pair(q):
+            w_rows_of[q] = row_pair()
             nc.sync.dma_start(
-                out=wih_sb[:, t0 : t0 + count, :],
-                in_=weight_ih[t0 * P : (t0 + count) * P, :].rearrange("(t p) k -> p t k", p=P),
+                out=w_rows_of[q][:],
+                in_=weight_ih[PAIR * q * P : PAIR * (q + 1) * P, :].rearrange("(t p) k -> p t k", p=P),
             )
 
-        def load_x(first, count):
-            nc.sync.dma_start(out=x_sb[:, first : first + count, :], in_=x_view[:, first : first + count, :])
+        def load_x_pair(q):
+            x_rows_of[q] = row_pair()
+            nc.sync.dma_start(out=x_rows_of[q][:], in_=x_view[:, PAIR * q : PAIR * (q + 1), :])
 
-        def load_acts(first, count, which=(0, 1, 2, 3)):
+        def load_acts(first, count, which):
             rows = slice(first, first + count)
             for s in which:
                 nc.sync.dma_start(out=acts_sb[:, s, rows, :], in_=act_views[s][:, rows, :])
 
-        load_acts(0, 2, (0,))
-        nc.sync.dma_start(
-            out=wplain_sb[:, 0:8, :], in_=weight_hh.rearrange("(t p) k -> p t k", p=P)
-        )
-        load_x(0, 2)
-        for t in range(0, 8, 2):
-            load_weight_tiles(t, 2)
-        nc.sync.dma_start(out=c_sb[:], in_=c_view)
-        for j, w in enumerate((weight_sh0, weight_sh1, weight_sh2)):
+        def load_plain_weight(t0, w):
+            n = w.shape[0] // P
             nc.sync.dma_start(
-                out=wplain_sb[:, 8 + 2 * j : 10 + 2 * j, :],
-                in_=w.rearrange("(t p) k -> p t k", p=P),
+                out=wplain_sb[:, t0 : t0 + n, :], in_=w.rearrange("(t p) k -> p t k", p=P)
             )
-        load_acts(0, 2, (1, 2, 3))
-        load_x(2, 2)
-        load_acts(2, 2)
-        for t in range(8, 14, 2):
-            load_weight_tiles(t, 2)
-        load_x(4, 4)
-        load_acts(4, 4)
+
+        load_x_pair(0)
+        load_plain_weight(0, weight_hh)
+        load_weight_pair(0)
+        load_x_pair(1)
+        load_weight_pair(1)
+        load_weight_pair(2)
+        load_weight_pair(3)
+        load_acts(0, 4, (0, 1, 2, 3))
+        for j, w in enumerate((weight_sh0, weight_sh1, weight_sh2)):
+            load_plain_weight(CORE_TILES + 2 * j, w)
+        nc.sync.dma_start(out=c_sb[:], in_=c_view)
 
         def copy_out(engine, out, in_):
             if engine == "S":
@@ -139,14 +151,25 @@ def tile_share_lstm_cell_pa_kernel(
             out = wplain_t[:].rearrange("p n e -> p (n e)").bitcast(F32)
             copy_out(engine, out[:, t0 * P : (t0 + count) * P], bank[:, 0:count, :].rearrange("p t n -> p (t n)"))
 
-        def broadcast_bias():
-            for c0, n in CHUNKS:
-                if c0 < BIAS_IN_PSUM_FROM:
-                    acc = psum.tile([P, BANK], F32, name="acc_bias", tag="bank")
-                    nc.tensor.matmul(
-                        acc[:, 0:n], lhsT=ones[:], rhs=bias_rows[:, c0 : c0 + n], start=True, stop=True
-                    )
-                    nc.vector.tensor_copy(out=bias_bc[:, c0 : c0 + n], in_=acc[:, 0:n])
+        acts_t_of = {}
+
+        def prepare_acts(r, which, engine):
+            if r not in acts_t_of:
+                acts_t_of[r] = stage.tile([P, 4, P, 2], BF16, name="acts_t", bufs=3)
+            words = acts_sb[:].bitcast(F32)
+            bank = psum.tile([P, 4, P], F32, name="bank_a", tag="bank")
+            for j, s in enumerate(which):
+                nc.tensor.transpose(bank[:, j, :], words[:, s, r, :], ident_f[:])
+            out = acts_t_of[r][:].rearrange("p s b e -> p s (b e)").bitcast(F32)
+            copy_out(engine, out[:, which[0] : which[-1] + 1, :], bank[:, 0 : len(which), :])
+
+        def transpose_bias():
+            bank = psum.tile([P, P], BF16, name="bank_b", tag="bank")
+            nc.tensor.transpose(bank[:], bias_rows[:], ident_bf[:])
+            nc.vector.tensor_copy(out=bias_cols[:], in_=bank[:, 0:64])
+            nc.vector.tensor_tensor(
+                out=bias[:], in0=bias_cols[:, 0:W_TILES], in1=bias_cols[:, 32 : 32 + W_TILES], op=ALU.add
+            )
 
         def regroup(engine, rows_bf16, grouped_words):
             words = rows_bf16.bitcast(F32)
@@ -158,167 +181,155 @@ def tile_share_lstm_cell_pa_kernel(
                     )
             copy_out(engine, grouped_words, bank[:].rearrange("p g u n -> p g n u"))
 
-        w_grouped_of = {}
-
-        def weight_tile(t, engine):
-            q, i = divmod(t, 2)
-            if i == 0:
-                w_grouped_of[q] = stage.tile([P, PASSES, 2 * P, 4], BF16, align_bytes=64, name="w_grouped")
-            words = w_grouped_of[q][:].bitcast(F32)
-            regroup(engine, wih_sb[:, t, :], words[:, :, i * P : (i + 1) * P, :])
-
-        def quantise_weights(q):
-            cols = slice(2 * P * q, 2 * P * (q + 1))
+        def quantise(grouped, codes, scales):
             for g in range(PASSES):
                 nc.vector.quantize_mx(
-                    out=w_codes[:, g, cols].bitcast(FP8X4),
-                    scales=w_scales[:, g, cols],
-                    in_=w_grouped_of[q][:, g, :, :].rearrange("p n t -> p (n t)"),
+                    out=codes[:, g, :].bitcast(FP8X4),
+                    scales=scales[:, g, :],
+                    in_=grouped[:, g, :, :].rearrange("p n t -> p (n t)"),
                 )
 
+        def tile_of_pair(grouped, i):
+            return grouped[:].bitcast(F32)[:, :, i * P : (i + 1) * P, :]
+
+        w_grouped_of = {}
         x_grouped_of = {}
-        acts_t_of = {}
+
+        def grouped_pair():
+            return stage.tile([P, PASSES, PAIR * P, 4], BF16, align_bytes=64, name="grouped", bufs=GROUP_BUFS)
+
+        def prepare_weights(t, engine):
+            q, i = divmod(t, PAIR)
+            if i == 0:
+                w_grouped_of[q] = grouped_pair()
+            regroup(engine, w_rows_of[q][:, i, :], tile_of_pair(w_grouped_of[q], i))
+
+        def quantise_weights(q):
+            cols = slice(PAIR * P * q, PAIR * P * (q + 1))
+            quantise(w_grouped_of[q], w_codes[:, :, cols], w_scales[:, :, cols])
 
         def prepare_x(r, engine):
-            x_grouped_of[r] = stage.tile([P, PASSES, P, 4], BF16, align_bytes=64, name="x_grouped")
-            regroup(engine, x_sb[:, r, :], x_grouped_of[r][:].bitcast(F32))
+            q, i = divmod(r, PAIR)
+            if i == 0:
+                x_grouped_of[q] = grouped_pair()
+            regroup(engine, x_rows_of[q][:, i, :], tile_of_pair(x_grouped_of[q], i))
 
-        def quantise_x(r):
-            nc.vector.quantize_mx(
-                out=x_codes[:, r, :, :].rearrange("p g b -> p (g b)").bitcast(FP8X4),
-                scales=x_scales[:, r, :, :].rearrange("p g b -> p (g b)"),
-                in_=x_grouped_of[r][:].rearrange("p g b t -> p (g b t)"),
-            )
+        def quantise_x(q):
+            half, i = divmod(q, TILES_PER_HALF // PAIR)
+            cols = slice(PAIR * P * i, PAIR * P * (i + 1))
+            quantise(x_grouped_of[q], x_codes[:, half, :, cols], x_scales[:, half, :, cols])
 
-        def prepare_acts(r, which, engine):
-            if r not in acts_t_of:
-                acts_t_of[r] = stage.tile([P, 4, P, 2], BF16, name="acts_t", bufs=4)
-            words = acts_sb[:].bitcast(F32)
-            bank = psum.tile([P, 4, P], F32, name="bank_a", tag="bank")
-            for j, s in enumerate(which):
-                nc.tensor.transpose(bank[:, j, :], words[:, s, r, :], ident_f[:])
-            out = acts_t_of[r][:].rearrange("p s b e -> p s (b e)").bitcast(F32)
-            copy_out(engine, out[:, which[0] : which[-1] + 1, :], bank[:, 0 : len(which), :])
+        mx_of = {}
 
-        gates_of = {}
-
-        def gate_cols(r, lo, hi):
-            shift = 0 if lo < 4 * DH else DH
-            return gates_of[r][:, lo + shift : hi + shift]
-
-
-        def plain(r, j, engine):
-            if r not in gates_of:
-                gates_of[r] = gate_pool.tile([P, GATES + DH], F32, name="gates")
-            c0, n = CHUNKS[j]
-            gates = gate_cols(r, c0, c0 + n)
-            bias_in_psum = engine == "S"
-            acc = psum.tile([P, BANK], F32, name="acc_plain", tag="bank")
-            for g0, width, s in PLAIN_GROUPS:
-                if c0 <= g0 < c0 + n:
-                    cols = acc[:, g0 - c0 : g0 - c0 + width]
-                    for e in range(2):
-                        nc.tensor.matmul(
-                            cols,
-                            lhsT=acts_t_of[r][:, s, :, e],
-                            rhs=wplain_t[:, g0 : g0 + width, e],
-                            start=(e == 0),
-                            stop=(e == 1 and not bias_in_psum),
-                        )
-                    if bias_in_psum:
-                        nc.tensor.matmul(
-                            cols, lhsT=ones[:], rhs=bias_rows[:, g0 : g0 + width], start=False, stop=True
-                        )
-            if bias_in_psum:
-                nc.scalar.copy(out=gates, in_=acc[:, 0:n])
-            else:
-                nc.vector.tensor_tensor(out=gates, in0=acc[:, 0:n], in1=bias_bc[:, c0 : c0 + n], op=ALU.add)
-
-        acc_of = {}
-
-        def mx(r, j):
-            c0, n = CHUNKS[j]
-            acc = psum.tile([P, BANK], F32, name="acc_mx", tag="bank")
-            acc_of[r, j] = acc
+        def mx(t, half, engine):
+            acc = psum.tile([P, HALF], F32, name="acc_mx", tag="bank")
+            rows = slice(t * P, (t + 1) * P)
             for g in range(PASSES):
                 nc.tensor.matmul_mx(
-                    out=acc[:, 0:n],
-                    lhsT=x_codes[:, r, g, :].bitcast(FP8X4),
-                    lhsT_scale=x_scales[:, r, g, :],
-                    rhs=w_codes[:, g, c0 : c0 + n].bitcast(FP8X4),
-                    rhs_scale=w_scales[:, g, c0 : c0 + n],
+                    out=acc[:],
+                    lhsT=w_codes[:, g, rows].bitcast(FP8X4),
+                    lhsT_scale=w_scales[:, g, rows],
+                    rhs=x_codes[:, half, g, :].bitcast(FP8X4),
+                    rhs_scale=x_scales[:, half, g, :],
                     start=(g == 0),
                     stop=(g == PASSES - 1),
                 )
+            mx_of[t, half] = stage.tile([P, HALF], F32, name="mx_t%d" % t)
+            out = mx_of[t, half][:]
+            if engine == "S":
+                nc.scalar.activation(out=out, in_=acc[:], func=ACT.Identity, bias=bias[:, t : t + 1])
+            else:
+                nc.vector.tensor_scalar(out=out, in0=acc[:], scalar1=bias[:, t : t + 1], scalar2=None, op0=ALU.add)
 
-        def add_mx(r, j):
-            c0, n = CHUNKS[j]
-            gates = gate_cols(r, c0, c0 + n)
-            nc.vector.tensor_tensor(out=gates, in0=acc_of[r, j][:, 0:n], in1=gates, op=ALU.add)
+        gates_of = {}
 
-        def squash(r, lo, hi, func):
-            gates = gate_cols(r, lo, hi)
-            nc.scalar.activation(out=gates, in_=gates, func=func)
+        def part(r, name):
+            half, i = divmod(r, TILES_PER_HALF)
+            acc = psum.tile([P, HALF], F32, name="acc_part", tag="bank")
+            at = 0
+            for g0, width, s in PARTS[name]:
+                for e in range(2):
+                    nc.tensor.matmul(
+                        acc[:, at : at + width],
+                        lhsT=acts_t_of[r][:, s, :, e],
+                        rhs=wplain_t[:, g0 : g0 + width, e],
+                        start=(e == 0),
+                        stop=False,
+                    )
+                for j in range(width // P):
+                    nc.tensor.matmul(
+                        acc[:, at + j * P : at + (j + 1) * P],
+                        lhsT=mx_of[g0 // P + j, half][:, i * P : (i + 1) * P],
+                        rhs=ident_f[:],
+                        is_transpose=True,
+                        start=False,
+                        stop=(j == width // P - 1),
+                    )
+                at += width
+            return acc[:, 0:at]
 
-        def squash_core(r):
-            squash(r, 0, 3 * DH, ACT.Sigmoid)
-            squash(r, 3 * DH, 4 * DH, ACT.Tanh)
+        I, F, O, C_HAT, MC, B0, B1, B2 = range(8)
 
-        def squash_shared(r):
-            squash(r, 4 * DH, 7 * DH, ACT.Sigmoid)
+        def gate(r, first, count=1):
+            return gates_of[r][:, first : first + count, :]
 
-        prod_of = {}
-        outs_of = {}
-        t_cell_of = {}
+        def new_gates(r):
+            gates_of[r] = gate_pool.tile([P, 8, DH], F32, name="gates")
 
-        def gate(r, k):
-            return gate_cols(r, k * DH, (k + 1) * DH)
+        def squash(r, name):
+            gates, func = {
+                "i f": (gate(r, I, 2), ACT.Sigmoid),
+                "c_hat": (gate(r, C_HAT), ACT.Tanh),
+                "o b2": (gates_of[r][:, O : B2 + 1 : B2 - O, :], ACT.Sigmoid),
+                "b0 b1": (gate(r, B0, 2), ACT.Sigmoid),
+            }[name]
+            nc.scalar.activation(out=gates, in_=part(r, name).rearrange("p (k d) -> p k d", d=DH), func=func)
 
         def row_mask(r):
             return mask_f[:, r : r + 1]
 
         def mask_c(r):
             nc.scalar.activation(
-                out=gates_of[r][:, 4 * DH : 5 * DH], in_=c_sb[:, r, :], func=ACT.Copy, scale=row_mask(r)
+                out=gate(r, MC), in_=c_sb[:, r : r + 1, :], func=ACT.Copy, scale=row_mask(r)
             )
 
+        prod_of = {}
+        outs_of = {}
+        t_cell_of = {}
+        e_of = {}
+
         def products(r):
-            prod_of[r] = work.tile([P, 2 * DH], F32, name="prod")
+            prod_of[r] = work.tile([P, 2, DH], F32, name="prod")
             nc.vector.tensor_tensor(
-                out=prod_of[r][:], in0=gates_of[r][:, 0 : 2 * DH], in1=gates_of[r][:, 3 * DH : 5 * DH], op=ALU.mult
+                out=prod_of[r][:], in0=gate(r, I, 2), in1=gate(r, C_HAT, 2), op=ALU.mult
             )
 
         def store(r, k):
             nc.sync.dma_start(out=out_views[k][:, r, :], in_=outs_of[r][:, SLOT[k], :])
 
         def cell(r):
-            outs_of[r] = work.tile([P, 5, DH], F32, name="outs")
+            outs_of[r] = work.tile([P, 5, DH], F32, name="outs", bufs=4)
             nc.vector.scalar_tensor_tensor(
-                out=outs_of[r][:, SLOT[1], :], in0=prod_of[r][:, 0:DH], scalar=row_mask(r),
-                in1=prod_of[r][:, DH : 2 * DH], op0=ALU.mult, op1=ALU.add,
+                out=outs_of[r][:, SLOT[1], :], in0=prod_of[r][:, 0, :], scalar=row_mask(r),
+                in1=prod_of[r][:, 1, :], op0=ALU.mult, op1=ALU.add,
             )
             store(r, 1)
 
         def tanh_cell(r):
-            t_cell_of[r] = work.tile([P, 2, DH], F32, name="t_cell")
-            nc.scalar.activation(out=t_cell_of[r][:, 1, :], in_=outs_of[r][:, SLOT[1], :], func=ACT.Tanh)
-
-        def mask_tanh(r):
-            nc.scalar.activation(
-                out=t_cell_of[r][:, 0, :], in_=t_cell_of[r][:, 1, :], func=ACT.Copy, scale=row_mask(r)
-            )
+            t_cell_of[r] = work.tile([P, 2, DH], F32, name="t_cell", bufs=4)
+            t_cell = t_cell_of[r]
+            nc.scalar.activation(out=t_cell[:, 1, :], in_=outs_of[r][:, SLOT[1], :], func=ACT.Tanh)
+            nc.scalar.activation(out=t_cell[:, 0, :], in_=t_cell[:, 1, :], func=ACT.Copy, scale=row_mask(r))
 
         def third_tanh(r):
             third = t_cell_of[r][:, 1, :]
             nc.scalar.activation(out=third, in_=third, func=ACT.Copy, scale=mask_third[:, r : r + 1])
 
         def minus_o(r):
-            b = gate_cols(r, 4 * DH, 7 * DH).rearrange("p (j d) -> p j d", j=3)
+            b = gate(r, B0, 3)
             nc.vector.tensor_tensor(
-                out=b, in0=b, in1=gate(r, 2).unsqueeze(1).to_broadcast([P, 3, DH]), op=ALU.subtract
+                out=b, in0=b, in1=gate(r, O).to_broadcast([P, 3, DH]), op=ALU.subtract
             )
-
-        e_of = {}
 
         def finish(r, *steps):
             stt = nc.vector.scalar_tensor_tensor
@@ -326,15 +337,16 @@ def tile_share_lstm_cell_pa_kernel(
             s0_out, s1_out = [outs_of[r][:, SLOT[k], :] for k in (2, 3)]
             if r not in e_of:
                 e_of[r] = work.tile([P, DH], F32, name="e1")
-            e1, e2 = e_of[r][:], gate(r, 3)
+            e1, e2 = e_of[r][:], gates_of[r][:, C_HAT, :]
+            b0, b1, b2 = [gates_of[r][:, b, :] for b in (B0, B1, B2)]
             for step in steps:
                 if step == 0:
-                    stt(out=s0_out, in0=gate(r, 4), scalar=1.0, in1=t_cell, op0=ALU.add, op1=ALU.mult)
+                    stt(out=s0_out, in0=b0, scalar=1.0, in1=t_cell, op0=ALU.add, op1=ALU.mult)
                     store(r, 2)
                 if step == 1:
-                    stt(out=e1, in0=gate(r, 5), scalar=2.0, in1=s0_out, op0=ALU.add, op1=ALU.subtract)
+                    stt(out=e1, in0=b1, scalar=2.0, in1=s0_out, op0=ALU.add, op1=ALU.subtract)
                 if step == 2:
-                    stt(out=e2, in0=s0_out, scalar=-2.0, in1=gate(r, 6), op0=ALU.mult, op1=ALU.add)
+                    stt(out=e2, in0=s0_out, scalar=-2.0, in1=b2, op0=ALU.mult, op1=ALU.add)
                 if step == 3:
                     stt(out=s1_out, in0=e1, scalar=0.5, in1=t_cell, op0=ALU.mult, op1=ALU.mult)
                     store(r, 3)
@@ -344,102 +356,138 @@ def tile_share_lstm_cell_pa_kernel(
         def first_and_last(r):
             nc.vector.tensor_tensor(
                 out=outs_of[r][:, 0:2, :],
-                in0=gates_of[r][:, 2 * DH : 4 * DH].rearrange("p (k d) -> p k d", k=2),
+                in0=gate(r, O, 2),
                 in1=t_cell_of[r][:],
                 op=ALU.mult,
             )
             store(r, 0)
             store(r, 4)
 
-
-        prepare_acts(0, (0,), "S")
-        plain_weights(0, 4, "V")
-        plain_weights(4, 4, "S")
-        prepare_x(0, "V")
-        quantise_x(0)
-        prepare_x(1, "S")
-        for t in range(4):
-            weight_tile(t, "SVSSSVSS"[t])
-            if t % 2 == 1:
-                quantise_weights(t // 2)
-        broadcast_bias()
-        plain(0, 0, "V")
-        plain(0, 1, "V")
-        mx(0, 0)
-        nc.vector.tensor_copy(out=mask_f[:], in_=mask_bf[:])
-        nc.vector.tensor_scalar(out=mask_third[:], in0=mask_f[:], scalar1=1.0 / 3.0, scalar2=None, op0=ALU.mult)
-        for t in range(4, 8):
-            weight_tile(t, "SVSSSVSS"[t])
-            if t % 2 == 1:
-                quantise_weights(t // 2)
-            if t == 5:
-                add_mx(0, 0)
-                mask_c(0)
-        quantise_x(1)
-        prepare_acts(0, (1, 2, 3), "S")
-        plain_weights(8, 4, "S")
-        plain_weights(12, 2, "S")
-
         def live(r):
             return 0 <= r < ROW_TILES
 
-        for n in range(ROW_TILES + 4):
-            if live(n + 1):
-                prepare_acts(n + 1, (0,), "S")
-            if live(n + 2):
-                prepare_x(n + 2, "S")
-            if live(n - 2):
-                tanh_cell(n - 2)
-                mask_tanh(n - 2)
-            if live(n) and n > 0:
-                plain(n, 0, "V")
-                plain(n, 1, "V")
-                mask_c(n)
-            if n == 1:
-                for t in (8, 9):
-                    weight_tile(t, "S" if t % 2 == 0 else "V")
-                quantise_weights(4)
-            if n == 1:
-                for t in (10, 11):
-                    weight_tile(t, "S" if t % 2 == 0 else "V")
-                quantise_weights(5)
-            if n == 1:
-                for t in (12, 13):
-                    weight_tile(t, "S" if t % 2 == 0 else "V")
-                quantise_weights(6)
-            if live(n - 1):
-                plain(n - 1, 2, "S")
-                plain(n - 1, 3, "S")
-            if live(n - 2):
-                third_tanh(n - 2)
-            if live(n):
-                if n > 0:
-                    mx(n, 0)
-                mx(n, 1)
-                if n > 0:
-                    add_mx(n, 0)
-                add_mx(n, 1)
-                squash_core(n)
-            if live(n - 1):
-                mx(n - 1, 2)
-                mx(n - 1, 3)
-                add_mx(n - 1, 2)
-                add_mx(n - 1, 3)
-                squash_shared(n - 1)
-            if live(n + 1):
-                prepare_acts(n + 1, (1, 2, 3), "S")
-            if live(n - 2):
-                minus_o(n - 2)
-            if live(n - 1):
-                products(n - 1)
-            if live(n - 2):
-                finish(n - 2, 0)
-            if live(n + 2):
-                quantise_x(n + 2)
-            if live(n - 2):
-                finish(n - 2, 1, 2, 3)
-            if live(n - 1):
-                cell(n - 1)
-            if live(n - 2):
-                finish(n - 2, 4)
-                first_and_last(n - 2)
+        prepare_x(0, "V")
+        prepare_x(1, "V")
+        quantise_x(0)
+        load_weight_pair(4)
+        plain_weights(0, 4, "S")
+        plain_weights(4, 4, "S")
+        prepare_weights(0, "V")
+        prepare_x(2, "S")
+        prepare_x(3, "V")
+        quantise_x(1)
+        prepare_weights(1, "S")
+        load_weight_pair(5)
+        quantise_weights(0)
+        transpose_bias()
+        prepare_weights(2, "S")
+        prepare_weights(3, "S")
+        load_weight_pair(6)
+        quantise_weights(1)
+        prepare_weights(4, "V")
+        prepare_weights(5, "S")
+        load_x_pair(2)
+        load_x_pair(3)
+        load_acts(4, 4, (0, 1, 2, 3))
+        quantise_weights(2)
+        prepare_weights(6, "S")
+        for t in range(6):
+            mx(t, 0, "SVSVSVVVSSVVVS"[t])
+        prepare_weights(7, "V")
+        quantise_weights(3)
+        nc.vector.tensor_copy(out=mask_f[:], in_=mask_bf[:])
+        nc.vector.tensor_scalar(out=mask_third[:], in0=mask_f[:], scalar1=1.0 / 3.0, scalar2=None, op0=ALU.mult)
+        prepare_acts(0, (0, 1, 2, 3), "S")
+        plain_weights(8, 4, "V")
+        plain_weights(12, 2, "S")
+        prepare_acts(1, (0, 1, 2, 3), "S")
+        new_gates(0)
+        mask_c(0)
+        prepare_weights(8, "S")
+        squash(0, "i f")
+        mx(6, 0, "V")
+        mx(7, 0, "V")
+        prepare_weights(9, "S")
+        quantise_weights(4)
+        prepare_weights(10, "V")
+        prepare_weights(11, "S")
+        squash(0, "c_hat")
+        prepare_weights(12, "V")
+        quantise_weights(5)
+        products(0)
+        prepare_weights(13, "S")
+        cell(0)
+        quantise_weights(6)
+        mx(8, 0, "S")
+        mx(9, 0, "S")
+        prepare_acts(2, (0, 1, 2, 3), "S")
+        tanh_cell(0)
+        new_gates(1)
+        mask_c(1)
+        squash(1, "i f")
+        for t in range(10, 14):
+            mx(t, 0, "SVSVSVVVSSVVVS"[t])
+
+        squash(0, "b0 b1")
+        squash(0, "o b2")
+        third_tanh(0)
+        squash(1, "c_hat")
+        products(1)
+        cell(1)
+        minus_o(0)
+        squash(1, "b0 b1")
+        squash(1, "o b2")
+        prepare_acts(3, (0, 1, 2, 3), "S")
+        X_LATE = "SSSS"
+        LATE = "SVSVSVSVSVSVSV"
+        late = []
+        def mx_late(count):
+            for t in range(len(late), min(len(late) + count, W_TILES)):
+                mx(t, 1, LATE[t])
+                late.append(t)
+        for half in range(HALVES):
+            first = half * TILES_PER_HALF
+            last = first + TILES_PER_HALF - 1
+            def within(r):
+                return first <= r <= last
+            for n in range(first + (2 if half == 0 else 0), last + 3):
+                if within(n):
+                    new_gates(n)
+                    mask_c(n)
+                    squash(n, "i f")
+                    squash(n, "c_hat")
+                if within(n - 1):
+                    tanh_cell(n - 1)
+                if within(n):
+                    squash(n, "b0 b1")
+                    squash(n, "o b2")
+                if within(n - 1):
+                    third_tanh(n - 1)
+                if n == 2:
+                    for r in range(4, 8):
+                        prepare_x(r, X_LATE[r - 4])
+                if half == 0 and n >= 4:
+                    mx_late(3)
+                if within(n) and live(n + 2):
+                    prepare_acts(n + 2, (0, 1, 2, 3), "S")
+                if within(n - 2):
+                    finish(n - 2, 0, 1, 2, 3)
+                if half == 0 and n >= 4:
+                    mx_late(4)
+                if within(n - 1) and n > 2:
+                    minus_o(n - 1)
+                if within(n - 2):
+                    finish(n - 2, 4)
+                if within(n):
+                    products(n)
+                if within(n - 2):
+                    first_and_last(n - 2)
+                if within(n):
+                    cell(n)
+                if n == 2:
+                    minus_o(1)
+                if n == 2:
+                    quantise_x(2)
+                    quantise_x(3)
+                if half == 0 and n >= 4:
+                    mx_late(7)

@@ -243,30 +243,34 @@ def tile_share_lstm_cell_pa_kernel(
 
         gates_of = {}
 
-        def part(r, name):
+        def parts(r, names):
             half, i = divmod(r, TILES_PER_HALF)
-            acc = psum.tile([P, HALF], F32, name="acc_part", tag="bank")
-            at = 0
-            for g0, width, s in PARTS[name]:
-                for e in range(2):
+            accs = {}
+            for name in names:
+                accs[name] = psum.tile([P, HALF], F32, name="acc_part", tag="bank")
+                at = 0
+                for g0, width, s in PARTS[name]:
+                    for e in range(2):
+                        nc.tensor.matmul(
+                            accs[name][:, at : at + width],
+                            lhsT=acts_t_of[r][:, s, :, e],
+                            rhs=wplain_t[:, g0 : g0 + width, e],
+                            start=(at == 0 and e == 0),
+                            stop=False,
+                        )
+                    at += width
+            for name in names:
+                tiles = [g0 // P + j for g0, width, s in PARTS[name] for j in range(width // P)]
+                for at, t in enumerate(tiles):
                     nc.tensor.matmul(
-                        acc[:, at : at + width],
-                        lhsT=acts_t_of[r][:, s, :, e],
-                        rhs=wplain_t[:, g0 : g0 + width, e],
-                        start=(e == 0),
-                        stop=False,
-                    )
-                for j in range(width // P):
-                    nc.tensor.matmul(
-                        acc[:, at + j * P : at + (j + 1) * P],
-                        lhsT=mx_of[g0 // P + j, half][:, i * P : (i + 1) * P],
+                        accs[name][:, at * P : (at + 1) * P],
+                        lhsT=mx_of[t, half][:, i * P : (i + 1) * P],
                         rhs=ident_f[:],
                         is_transpose=True,
                         start=False,
-                        stop=(j == width // P - 1),
+                        stop=(at == len(tiles) - 1),
                     )
-                at += width
-            return acc[:, 0:at]
+            return accs
 
         I, F, O, C_HAT, MC, B0, B1, B2 = range(8)
 
@@ -276,14 +280,20 @@ def tile_share_lstm_cell_pa_kernel(
         def new_gates(r):
             gates_of[r] = gate_pool.tile([P, 8, DH], F32, name="gates")
 
-        def squash(r, name):
-            gates, func = {
+        def squash(r, *names):
+            accs = parts(r, names)
+            gates_and_func = {
                 "i f": (gate(r, I, 2), ACT.Sigmoid),
                 "c_hat": (gate(r, C_HAT), ACT.Tanh),
                 "o b2": (gates_of[r][:, O : B2 + 1 : B2 - O, :], ACT.Sigmoid),
                 "b0 b1": (gate(r, B0, 2), ACT.Sigmoid),
-            }[name]
-            nc.scalar.activation(out=gates, in_=part(r, name).rearrange("p (k d) -> p k d", d=DH), func=func)
+            }
+            for name in names:
+                gates, func = gates_and_func[name]
+                width = sum(run[1] for run in PARTS[name])
+                nc.scalar.activation(
+                    out=gates, in_=accs[name][:, 0:width].rearrange("p (k d) -> p k d", d=DH), func=func
+                )
 
         def row_mask(r):
             return mask_f[:, r : r + 1]
@@ -428,18 +438,16 @@ def tile_share_lstm_cell_pa_kernel(
         for t in range(10, 14):
             mx(t, 0, "SVSVSVVVSSVVVS"[t])
 
-        squash(0, "b0 b1")
-        squash(0, "o b2")
+        squash(0, "b0 b1", "o b2")
         third_tanh(0)
         squash(1, "c_hat")
         products(1)
         cell(1)
         minus_o(0)
-        squash(1, "b0 b1")
-        squash(1, "o b2")
+        squash(1, "b0 b1", "o b2")
         prepare_acts(3, (0, 1, 2, 3), "S")
         X_LATE = "SSSS"
-        LATE = "SVSVSVSVSVSVSV"
+        LATE = "SSVSSVSSVSSVSS"
         late = []
         def mx_late(count):
             for t in range(len(late), min(len(late) + count, W_TILES)):
@@ -454,13 +462,11 @@ def tile_share_lstm_cell_pa_kernel(
                 if within(n):
                     new_gates(n)
                     mask_c(n)
-                    squash(n, "i f")
-                    squash(n, "c_hat")
+                    squash(n, "i f", "c_hat")
                 if within(n - 1):
                     tanh_cell(n - 1)
                 if within(n):
-                    squash(n, "b0 b1")
-                    squash(n, "o b2")
+                    squash(n, "b0 b1", "o b2")
                 if within(n - 1):
                     third_tanh(n - 1)
                 if n == 2:

@@ -110,14 +110,21 @@ def tile_share_lstm_cell_pa_kernel(
                 in_=weight_ih[PAIR * q * P : PAIR * (q + 1) * P, :].rearrange("(t p) k -> p t k", p=P),
             )
 
-        def load_x_pair(q):
+        def load_x_pair(q, pieces=1):
             x_rows_of[q] = row_pair()
-            nc.sync.dma_start(out=x_rows_of[q][:], in_=x_view[:, PAIR * q : PAIR * (q + 1), :])
+            step = PAIR // pieces
+            for i in range(0, PAIR, step):
+                first = PAIR * q + i
+                nc.sync.dma_start(out=x_rows_of[q][:, i : i + step, :], in_=x_view[:, first : first + step, :])
 
         def load_acts(first, count, which):
             rows = slice(first, first + count)
             for s in which:
                 nc.sync.dma_start(out=acts_sb[:, s, rows, :], in_=act_views[s][:, rows, :])
+
+        def load_c(first, count):
+            rows = slice(first, first + count)
+            nc.sync.dma_start(out=c_sb[:, rows, :], in_=c_view[:, rows, :])
 
         def load_plain_weight(t0, w):
             n = w.shape[0] // P
@@ -125,17 +132,15 @@ def tile_share_lstm_cell_pa_kernel(
                 out=wplain_sb[:, t0 : t0 + n, :], in_=w.rearrange("(t p) k -> p t k", p=P)
             )
 
-        load_x_pair(0)
+        load_x_pair(0, pieces=2)
         load_plain_weight(0, weight_hh)
         load_weight_pair(0)
         load_x_pair(1)
         load_weight_pair(1)
         load_weight_pair(2)
         load_weight_pair(3)
-        load_acts(0, 4, (0, 1, 2, 3))
-        for j, w in enumerate((weight_sh0, weight_sh1, weight_sh2)):
-            load_plain_weight(CORE_TILES + 2 * j, w)
-        nc.sync.dma_start(out=c_sb[:], in_=c_view)
+        load_acts(0, 4, (0,))
+        load_c(0, 4)
 
         def copy_out(engine, out, in_):
             if engine == "S":
@@ -248,18 +253,6 @@ def tile_share_lstm_cell_pa_kernel(
             accs = {}
             for name in names:
                 accs[name] = psum.tile([P, HALF], F32, name="acc_part", tag="bank")
-                at = 0
-                for g0, width, s in PARTS[name]:
-                    for e in range(2):
-                        nc.tensor.matmul(
-                            accs[name][:, at : at + width],
-                            lhsT=acts_t_of[r][:, s, :, e],
-                            rhs=wplain_t[:, g0 : g0 + width, e],
-                            start=(at == 0 and e == 0),
-                            stop=False,
-                        )
-                    at += width
-            for name in names:
                 tiles = [g0 // P + j for g0, width, s in PARTS[name] for j in range(width // P)]
                 for at, t in enumerate(tiles):
                     nc.tensor.matmul(
@@ -267,9 +260,22 @@ def tile_share_lstm_cell_pa_kernel(
                         lhsT=mx_of[t, half][:, i * P : (i + 1) * P],
                         rhs=ident_f[:],
                         is_transpose=True,
-                        start=False,
-                        stop=(at == len(tiles) - 1),
+                        start=(at == 0),
+                        stop=False,
                     )
+            for name in names:
+                at = 0
+                runs = PARTS[name]
+                for g0, width, s in runs:
+                    for e in range(2):
+                        nc.tensor.matmul(
+                            accs[name][:, at : at + width],
+                            lhsT=acts_t_of[r][:, s, :, e],
+                            rhs=wplain_t[:, g0 : g0 + width, e],
+                            start=False,
+                            stop=(e == 1 and g0 == runs[-1][0]),
+                        )
+                    at += width
             return accs
 
         I, F, O, C_HAT, MC, B0, B1, B2 = range(8)
@@ -393,12 +399,16 @@ def tile_share_lstm_cell_pa_kernel(
         prepare_weights(2, "S")
         prepare_weights(3, "S")
         load_weight_pair(6)
+        load_acts(0, 4, (1, 2, 3))
+        for j, w in enumerate((weight_sh0, weight_sh1, weight_sh2)):
+            load_plain_weight(CORE_TILES + 2 * j, w)
         quantise_weights(1)
         prepare_weights(4, "V")
         prepare_weights(5, "S")
         load_x_pair(2)
         load_x_pair(3)
         load_acts(4, 4, (0, 1, 2, 3))
+        load_c(4, 4)
         quantise_weights(2)
         prepare_weights(6, "S")
         for t in range(6):
@@ -407,10 +417,8 @@ def tile_share_lstm_cell_pa_kernel(
         quantise_weights(3)
         nc.vector.tensor_copy(out=mask_f[:], in_=mask_bf[:])
         nc.vector.tensor_scalar(out=mask_third[:], in0=mask_f[:], scalar1=1.0 / 3.0, scalar2=None, op0=ALU.mult)
-        prepare_acts(0, (0, 1, 2, 3), "S")
-        plain_weights(8, 4, "V")
-        plain_weights(12, 2, "S")
-        prepare_acts(1, (0, 1, 2, 3), "S")
+        prepare_acts(0, (0,), "S")
+        prepare_acts(1, (0,), "S")
         new_gates(0)
         mask_c(0)
         prepare_weights(8, "S")
@@ -428,10 +436,14 @@ def tile_share_lstm_cell_pa_kernel(
         prepare_weights(13, "S")
         cell(0)
         quantise_weights(6)
+        plain_weights(8, 4, "V")
+        plain_weights(12, 2, "S")
+        prepare_acts(0, (1, 2, 3), "S")
         mx(8, 0, "S")
         mx(9, 0, "S")
         prepare_acts(2, (0, 1, 2, 3), "S")
         tanh_cell(0)
+        prepare_acts(1, (1, 2, 3), "S")
         new_gates(1)
         mask_c(1)
         squash(1, "i f")

@@ -84,16 +84,16 @@ def tile_share_lstm_cell_pa_kernel(
         make_identity(nc, ident_f[:])
         make_identity(nc, ident_bf[:])
 
-        def load_bias(first_row, vec):
+        def load_bias(engine, first_row, vec):
             n = vec.shape[0] // P
-            nc.scalar.dma_start(
+            engine.dma_start(
                 out=bias_rows[first_row : first_row + n, :], in_=vec.rearrange("(t n) -> t n", n=P)
             )
 
-        load_bias(0, bias_ih)
-        load_bias(32, bias_hh)
+        load_bias(nc.scalar, 0, bias_ih)
+        load_bias(nc.scalar, 32, bias_hh)
         for j, b in enumerate((bias_sh0, bias_sh1, bias_sh2)):
-            load_bias(32 + CORE_TILES + 2 * j, b)
+            load_bias(nc.gpsimd, 32 + CORE_TILES + 2 * j, b)
         nc.scalar.activation(out=warm[:], in_=warm[:], func=ACT.Sigmoid)
         nc.gpsimd.dma_start(out=mask_bf[:], in_=mask.rearrange("(p r) -> p r", r=ROW_TILES))
 
@@ -132,7 +132,7 @@ def tile_share_lstm_cell_pa_kernel(
                 out=wplain_sb[:, t0 : t0 + n, :], in_=w.rearrange("(t p) k -> p t k", p=P)
             )
 
-        load_x_pair(0, pieces=2)
+        load_x_pair(0)
         load_plain_weight(0, weight_hh)
         load_weight_pair(0)
         load_x_pair(1)
@@ -395,7 +395,6 @@ def tile_share_lstm_cell_pa_kernel(
         prepare_weights(1, "S")
         load_weight_pair(5)
         quantise_weights(0)
-        transpose_bias()
         prepare_weights(2, "S")
         prepare_weights(3, "S")
         load_weight_pair(6)
@@ -410,6 +409,7 @@ def tile_share_lstm_cell_pa_kernel(
         load_acts(4, 4, (0, 1, 2, 3))
         load_c(4, 4)
         quantise_weights(2)
+        transpose_bias()
         prepare_weights(6, "S")
         for t in range(6):
             mx(t, 0, "SVSVSVVVSSVVVS"[t])

@@ -21,19 +21,19 @@ W_TILES = GATES // P
 CORE_TILES = 4 * DH // P
 K_PASS = 4 * P
 PASSES = DI // K_PASS
+PAIR = 2
 ROW_BUFS = 6
 GROUP_BUFS = 3
-PAIR = 2
 HALF = 512
 HALVES = BATCH // HALF
 TILES_PER_HALF = HALF // P
+SCALAR, VECTOR = "Scalar", "Vector"
 PARTS = {
     "i f": ((0, 2 * DH, 0),),
     "c_hat": ((3 * DH, DH, 0),),
     "o b2": ((2 * DH, DH, 0), (6 * DH, DH, 3)),
     "b0 b1": ((4 * DH, DH, 1), (5 * DH, DH, 2)),
 }
-SLOT = (0, 2, 3, 4, 1)
 
 FLOPS = 2 * BATCH * (GATES * DI + 4 * DH * DH + 3 * DH * DH)
 
@@ -64,13 +64,12 @@ def tile_share_lstm_cell_pa_kernel(
         acts_sb = keep.tile([P, 4, ROW_TILES, DH], BF16)
         c_sb = keep.tile([P, ROW_TILES, DH], BF16)
         wplain_sb = keep.tile([P, W_TILES, DH], BF16)
-        wplain_t = keep.tile([P, GATES, 2], BF16)
+        wplain_t = keep.tile([P, 2, GATES], BF16)
         bias_rows = keep.tile([P, P], BF16)
         bias_cols = keep.tile([P, 64], F32)
         bias = keep.tile([P, W_TILES], F32)
         mask_bf = keep.tile([P, ROW_TILES], BF16)
         mask_f = keep.tile([P, ROW_TILES], F32)
-        mask_third = keep.tile([P, ROW_TILES], F32)
         ident_bf = keep.tile([P, P], BF16)
         ident_f = keep.tile([P, P], F32)
         warm = keep.tile([P, 1], F32)
@@ -110,12 +109,9 @@ def tile_share_lstm_cell_pa_kernel(
                 in_=weight_ih[PAIR * q * P : PAIR * (q + 1) * P, :].rearrange("(t p) k -> p t k", p=P),
             )
 
-        def load_x_pair(q, pieces=1):
+        def load_x_pair(q):
             x_rows_of[q] = row_pair()
-            step = PAIR // pieces
-            for i in range(0, PAIR, step):
-                first = PAIR * q + i
-                nc.sync.dma_start(out=x_rows_of[q][:, i : i + step, :], in_=x_view[:, first : first + step, :])
+            nc.sync.dma_start(out=x_rows_of[q][:], in_=x_view[:, PAIR * q : PAIR * (q + 1), :])
 
         def load_acts(first, count, which):
             rows = slice(first, first + count)
@@ -132,18 +128,18 @@ def tile_share_lstm_cell_pa_kernel(
                 out=wplain_sb[:, t0 : t0 + n, :], in_=w.rearrange("(t p) k -> p t k", p=P)
             )
 
+        H, S0, S1, S2 = range(4)
         load_x_pair(0)
         load_plain_weight(0, weight_hh)
         load_weight_pair(0)
         load_x_pair(1)
-        load_weight_pair(1)
-        load_weight_pair(2)
-        load_weight_pair(3)
-        load_acts(0, 4, (0,))
-        load_c(0, 4)
+        for q in range(1, 4):
+            load_weight_pair(q)
+        load_acts(0, TILES_PER_HALF, (H,))
+        load_c(0, TILES_PER_HALF)
 
         def copy_out(engine, out, in_):
-            if engine == "S":
+            if engine == SCALAR:
                 nc.scalar.copy(out=out, in_=in_)
             else:
                 nc.vector.tensor_copy(out=out, in_=in_)
@@ -153,8 +149,12 @@ def tile_share_lstm_cell_pa_kernel(
             words = wplain_sb[:].bitcast(F32)
             for t in range(count):
                 nc.tensor.transpose(bank[:, t, :], words[:, t0 + t, :], ident_f[:])
-            out = wplain_t[:].rearrange("p n e -> p (n e)").bitcast(F32)
-            copy_out(engine, out[:, t0 * P : (t0 + count) * P], bank[:, 0:count, :].rearrange("p t n -> p (t n)"))
+            pairs = bank[:, 0:count, :].rearrange("p t n -> p (t n)").bitcast(BF16)
+            copy_out(
+                engine,
+                wplain_t[:, :, t0 * P : (t0 + count) * P],
+                pairs.rearrange("p (n e) -> p e n", e=2),
+            )
 
         acts_t_of = {}
 
@@ -226,7 +226,8 @@ def tile_share_lstm_cell_pa_kernel(
 
         mx_of = {}
 
-        def mx(t, half, engine):
+        def mx(t, half):
+            engine = SCALAR if t % 2 == 0 else VECTOR
             acc = psum.tile([P, HALF], F32, name="acc_mx", tag="bank")
             rows = slice(t * P, (t + 1) * P)
             for g in range(PASSES):
@@ -241,7 +242,7 @@ def tile_share_lstm_cell_pa_kernel(
                 )
             mx_of[t, half] = stage.tile([P, HALF], F32, name="mx_t%d" % t)
             out = mx_of[t, half][:]
-            if engine == "S":
+            if engine == SCALAR:
                 nc.scalar.activation(out=out, in_=acc[:], func=ACT.Identity, bias=bias[:, t : t + 1])
             else:
                 nc.vector.tensor_scalar(out=out, in0=acc[:], scalar1=bias[:, t : t + 1], scalar2=None, op0=ALU.add)
@@ -271,7 +272,7 @@ def tile_share_lstm_cell_pa_kernel(
                         nc.tensor.matmul(
                             accs[name][:, at : at + width],
                             lhsT=acts_t_of[r][:, s, :, e],
-                            rhs=wplain_t[:, g0 : g0 + width, e],
+                            rhs=wplain_t[:, e, g0 : g0 + width],
                             start=False,
                             stop=(e == 1 and g0 == runs[-1][0]),
                         )
@@ -321,25 +322,21 @@ def tile_share_lstm_cell_pa_kernel(
             )
 
         def store(r, k):
-            nc.sync.dma_start(out=out_views[k][:, r, :], in_=outs_of[r][:, SLOT[k], :])
+            nc.sync.dma_start(out=out_views[k][:, r, :], in_=outs_of[r][:, k, :])
 
         def cell(r):
             outs_of[r] = work.tile([P, 5, DH], F32, name="outs", bufs=4)
             nc.vector.scalar_tensor_tensor(
-                out=outs_of[r][:, SLOT[1], :], in0=prod_of[r][:, 0, :], scalar=row_mask(r),
+                out=outs_of[r][:, 1, :], in0=prod_of[r][:, 0, :], scalar=row_mask(r),
                 in1=prod_of[r][:, 1, :], op0=ALU.mult, op1=ALU.add,
             )
             store(r, 1)
 
         def tanh_cell(r):
-            t_cell_of[r] = work.tile([P, 2, DH], F32, name="t_cell", bufs=4)
-            t_cell = t_cell_of[r]
-            nc.scalar.activation(out=t_cell[:, 1, :], in_=outs_of[r][:, SLOT[1], :], func=ACT.Tanh)
-            nc.scalar.activation(out=t_cell[:, 0, :], in_=t_cell[:, 1, :], func=ACT.Copy, scale=row_mask(r))
-
-        def third_tanh(r):
-            third = t_cell_of[r][:, 1, :]
-            nc.scalar.activation(out=third, in_=third, func=ACT.Copy, scale=mask_third[:, r : r + 1])
+            t_cell_of[r] = work.tile([P, DH], F32, name="t_cell", bufs=4)
+            t_cell = t_cell_of[r][:]
+            nc.scalar.activation(out=t_cell, in_=outs_of[r][:, 1, :], func=ACT.Tanh)
+            nc.scalar.activation(out=t_cell, in_=t_cell, func=ACT.Copy, scale=row_mask(r))
 
         def minus_o(r):
             b = gate(r, B0, 3)
@@ -347,13 +344,19 @@ def tile_share_lstm_cell_pa_kernel(
                 out=b, in0=b, in1=gate(r, O).to_broadcast([P, 3, DH]), op=ALU.subtract
             )
 
+        def hidden(r):
+            nc.vector.tensor_tensor(
+                out=outs_of[r][:, 0, :], in0=gates_of[r][:, O, :], in1=t_cell_of[r][:], op=ALU.mult
+            )
+            store(r, 0)
+
         def finish(r, *steps):
             stt = nc.vector.scalar_tensor_tensor
-            t_cell = t_cell_of[r][:, 0, :]
-            s0_out, s1_out = [outs_of[r][:, SLOT[k], :] for k in (2, 3)]
+            t_cell = t_cell_of[r][:]
+            s0_out, s1_out, s2_out = [outs_of[r][:, k, :] for k in (2, 3, 4)]
             if r not in e_of:
-                e_of[r] = work.tile([P, DH], F32, name="e1")
-            e1, e2 = e_of[r][:], gates_of[r][:, C_HAT, :]
+                e_of[r] = (work.tile([P, DH], F32, name="e1"), work.tile([P, DH], F32, name="e2"))
+            e1, e2 = [e[:] for e in e_of[r]]
             b0, b1, b2 = [gates_of[r][:, b, :] for b in (B0, B1, B2)]
             for step in steps:
                 if step == 0:
@@ -368,144 +371,140 @@ def tile_share_lstm_cell_pa_kernel(
                     store(r, 3)
                 if step == 4:
                     stt(out=e2, in0=e2, scalar=3.0, in1=s1_out, op0=ALU.add, op1=ALU.subtract)
+                if step == 5:
+                    stt(out=s2_out, in0=e2, scalar=1.0 / 3.0, in1=t_cell, op0=ALU.mult, op1=ALU.mult)
+                    store(r, 4)
 
-        def first_and_last(r):
-            nc.vector.tensor_tensor(
-                out=outs_of[r][:, 0:2, :],
-                in0=gate(r, O, 2),
-                in1=t_cell_of[r][:],
-                op=ALU.mult,
-            )
-            store(r, 0)
-            store(r, 4)
+        def core_gates(r):
+            new_gates(r)
+            mask_c(r)
+            squash(r, "i f", "c_hat")
 
-        def live(r):
-            return 0 <= r < ROW_TILES
+        def shared_gates(r):
+            squash(r, "b0 b1", "o b2")
 
-        prepare_x(0, "V")
-        prepare_x(1, "V")
+        def begin_outputs(r):
+            finish(r, 0)
+            hidden(r)
+
+        prepare_x(0, VECTOR)
+        prepare_x(1, VECTOR)
         quantise_x(0)
         load_weight_pair(4)
-        plain_weights(0, 4, "S")
-        plain_weights(4, 4, "S")
-        prepare_weights(0, "V")
-        prepare_x(2, "S")
-        prepare_x(3, "V")
+        plain_weights(0, 4, SCALAR)
+        plain_weights(4, 4, SCALAR)
+        prepare_weights(0, SCALAR)
+        prepare_x(2, VECTOR)
+        prepare_x(3, VECTOR)
         quantise_x(1)
-        prepare_weights(1, "S")
+        prepare_weights(1, SCALAR)
         load_weight_pair(5)
         quantise_weights(0)
-        prepare_weights(2, "S")
-        prepare_weights(3, "S")
+        prepare_weights(2, SCALAR)
+        prepare_weights(3, SCALAR)
         load_weight_pair(6)
-        load_acts(0, 4, (1, 2, 3))
+        load_acts(0, TILES_PER_HALF, (S0, S1, S2))
         for j, w in enumerate((weight_sh0, weight_sh1, weight_sh2)):
             load_plain_weight(CORE_TILES + 2 * j, w)
         quantise_weights(1)
-        prepare_weights(4, "V")
-        prepare_weights(5, "S")
+        prepare_weights(4, SCALAR)
+        prepare_weights(5, SCALAR)
         load_x_pair(2)
         load_x_pair(3)
-        load_acts(4, 4, (0, 1, 2, 3))
-        load_c(4, 4)
+        load_acts(TILES_PER_HALF, TILES_PER_HALF, (H, S0, S1, S2))
+        load_c(TILES_PER_HALF, TILES_PER_HALF)
         quantise_weights(2)
         transpose_bias()
-        prepare_weights(6, "S")
+        prepare_weights(6, SCALAR)
         for t in range(6):
-            mx(t, 0, "SVSVSVVVSSVVVS"[t])
-        prepare_weights(7, "V")
+            mx(t, 0)
+        prepare_weights(7, SCALAR)
         quantise_weights(3)
         nc.vector.tensor_copy(out=mask_f[:], in_=mask_bf[:])
-        nc.vector.tensor_scalar(out=mask_third[:], in0=mask_f[:], scalar1=1.0 / 3.0, scalar2=None, op0=ALU.mult)
-        prepare_acts(0, (0,), "S")
-        prepare_acts(1, (0,), "S")
+        prepare_acts(0, (H,), SCALAR)
+        prepare_acts(1, (H,), SCALAR)
+
         new_gates(0)
         mask_c(0)
-        prepare_weights(8, "S")
+        prepare_weights(8, SCALAR)
         squash(0, "i f")
-        mx(6, 0, "V")
-        mx(7, 0, "V")
-        prepare_weights(9, "S")
+        mx(6, 0)
+        mx(7, 0)
+        prepare_weights(9, SCALAR)
         quantise_weights(4)
-        prepare_weights(10, "V")
-        prepare_weights(11, "S")
+        prepare_weights(10, SCALAR)
+        prepare_weights(11, SCALAR)
         squash(0, "c_hat")
-        prepare_weights(12, "V")
+        prepare_weights(12, SCALAR)
         quantise_weights(5)
         products(0)
-        prepare_weights(13, "S")
+        prepare_weights(13, SCALAR)
         cell(0)
         quantise_weights(6)
-        plain_weights(8, 4, "V")
-        plain_weights(12, 2, "S")
-        prepare_acts(0, (1, 2, 3), "S")
-        mx(8, 0, "S")
-        mx(9, 0, "S")
-        prepare_acts(2, (0, 1, 2, 3), "S")
+        plain_weights(CORE_TILES, 4, VECTOR)
+        plain_weights(CORE_TILES + 4, 2, SCALAR)
+        prepare_acts(0, (S0, S1, S2), SCALAR)
+        mx(8, 0)
+        mx(9, 0)
+        prepare_acts(2, (H, S0, S1, S2), SCALAR)
         tanh_cell(0)
-        prepare_acts(1, (1, 2, 3), "S")
+        prepare_acts(1, (S0, S1, S2), SCALAR)
         new_gates(1)
         mask_c(1)
         squash(1, "i f")
-        for t in range(10, 14):
-            mx(t, 0, "SVSVSVVVSSVVVS"[t])
-
-        squash(0, "b0 b1", "o b2")
-        third_tanh(0)
+        for t in range(10, W_TILES):
+            mx(t, 0)
         squash(1, "c_hat")
         products(1)
         cell(1)
+        shared_gates(0)
         minus_o(0)
-        squash(1, "b0 b1", "o b2")
-        prepare_acts(3, (0, 1, 2, 3), "S")
-        X_LATE = "SSSS"
-        LATE = "SSVSSVSSVSSVSS"
-        late = []
-        def mx_late(count):
-            for t in range(len(late), min(len(late) + count, W_TILES)):
-                mx(t, 1, LATE[t])
-                late.append(t)
+        shared_gates(1)
+        prepare_acts(3, (H, S0, S1, S2), SCALAR)
+
         for half in range(HALVES):
             first = half * TILES_PER_HALF
             last = first + TILES_PER_HALF - 1
-            def within(r):
-                return first <= r <= last
-            for n in range(first + (2 if half == 0 else 0), last + 3):
-                if within(n):
-                    new_gates(n)
-                    mask_c(n)
-                    squash(n, "i f", "c_hat")
-                if within(n - 1):
+            for n in range(first + 2 if half == 0 else first, last + 3):
+                making = n <= last
+                finishing = n - 2 >= first
+                if making:
+                    core_gates(n)
+                if first <= n - 1 <= last:
                     tanh_cell(n - 1)
-                if within(n):
-                    squash(n, "b0 b1", "o b2")
-                if within(n - 1):
-                    third_tanh(n - 1)
+                if making:
+                    shared_gates(n)
                 if n == 2:
-                    for r in range(4, 8):
-                        prepare_x(r, X_LATE[r - 4])
-                if half == 0 and n >= 4:
-                    mx_late(3)
-                if within(n) and live(n + 2):
-                    prepare_acts(n + 2, (0, 1, 2, 3), "S")
-                if within(n - 2):
-                    finish(n - 2, 0, 1, 2, 3)
-                if half == 0 and n >= 4:
-                    mx_late(4)
-                if within(n - 1) and n > 2:
+                    for r in range(TILES_PER_HALF, ROW_TILES):
+                        prepare_x(r, SCALAR)
+                if n == TILES_PER_HALF and half == 0:
+                    for t in range(3):
+                        mx(t, 1)
+                if making and n + 2 < ROW_TILES:
+                    prepare_acts(n + 2, (H, S0, S1, S2), SCALAR)
+                if finishing:
+                    if n - 2 < last:
+                        begin_outputs(n - 2)
+                    finish(n - 2, 1, 2, 3)
+                if n == TILES_PER_HALF and half == 0:
+                    for t in range(3, 7):
+                        mx(t, 1)
+                if first <= n - 1 <= last and n > 2:
                     minus_o(n - 1)
-                if within(n - 2):
+                if finishing:
                     finish(n - 2, 4)
-                if within(n):
+                if n - 1 == last:
+                    begin_outputs(last)
+                if making:
                     products(n)
-                if within(n - 2):
-                    first_and_last(n - 2)
-                if within(n):
+                if finishing:
+                    finish(n - 2, 5)
+                if making:
                     cell(n)
                 if n == 2:
                     minus_o(1)
-                if n == 2:
                     quantise_x(2)
                     quantise_x(3)
-                if half == 0 and n >= 4:
-                    mx_late(7)
+                if n == TILES_PER_HALF and half == 0:
+                    for t in range(7, W_TILES):
+                        mx(t, 1)

from contextlib import ExitStack

import concourse.mybir as mybir
from concourse.masks import make_identity

F32 = mybir.dt.float32
BF16 = mybir.dt.bfloat16
U32 = mybir.dt.uint32
U8 = mybir.dt.uint8
FP8X4 = mybir.dt.float8_e4m3fn_x4
ACT = mybir.ActivationFunctionType
ALU = mybir.AluOpType

P = 128
BATCH = 1024
DI = 1024
DH = 256
GATES = 7 * DH
ROW_TILES = BATCH // P
W_TILES = GATES // P
CORE_TILES = 4 * DH // P
K_PASS = 4 * P
PASSES = DI // K_PASS
PAIR = 2
ROW_BUFS = 6
GROUP_BUFS = 3
HALF = 512
HALVES = BATCH // HALF
TILES_PER_HALF = HALF // P
SCALAR, VECTOR = "Scalar", "Vector"
PARTS = {
    "i f": ((0, 2 * DH, 0),),
    "c_hat": ((3 * DH, DH, 0),),
    "o b2": ((2 * DH, DH, 0), (6 * DH, DH, 3)),
    "b0 b1": ((4 * DH, DH, 1), (5 * DH, DH, 2)),
}

FLOPS = 2 * BATCH * (GATES * DI + 4 * DH * DH + 3 * DH * DH)


def tile_share_lstm_cell_pa_kernel(
    tc, x, h_minors, c_minors, s0, s1, s2, mask,
    weight_ih, bias_ih, weight_hh, bias_hh,
    weight_sh0, bias_sh0, weight_sh1, bias_sh1, weight_sh2, bias_sh2,
    out_0, out_1, out_2, out_3, out_4,
):
    nc = tc.nc
    with ExitStack() as ctx:
        keep = ctx.enter_context(tc.tile_pool(name="keep", bufs=1))
        stage = ctx.enter_context(tc.tile_pool(name="stage", bufs=2))
        gate_pool = ctx.enter_context(tc.tile_pool(name="gate_pool", bufs=4))
        work = ctx.enter_context(tc.tile_pool(name="work", bufs=2))
        psum = ctx.enter_context(tc.psum_pool(name="psum", bufs=8))
        ctx.enter_context(tc.manual_schedule())

        def by_row_tile(ap):
            return ap.rearrange("(p r) d -> p r d", r=ROW_TILES)

        x_view = by_row_tile(x)
        c_view = by_row_tile(c_minors)
        act_views = [by_row_tile(a) for a in (h_minors, s0, s1, s2)]
        out_views = [by_row_tile(o) for o in (out_0, out_1, out_2, out_3, out_4)]

        acts_sb = keep.tile([P, 4, ROW_TILES, DH], BF16)
        c_sb = keep.tile([P, ROW_TILES, DH], BF16)
        wplain_sb = keep.tile([P, W_TILES, DH], BF16)
        wplain_t = keep.tile([P, 2, GATES], BF16)
        bias_rows = keep.tile([P, P], BF16)
        bias_cols = keep.tile([P, 64], F32)
        bias = keep.tile([P, W_TILES], F32)
        mask_bf = keep.tile([P, ROW_TILES], BF16)
        mask_f = keep.tile([P, ROW_TILES], F32)
        ident_bf = keep.tile([P, P], BF16)
        ident_f = keep.tile([P, P], F32)
        warm = keep.tile([P, 1], F32)
        x_codes = keep.tile([P, HALVES, PASSES, HALF], U32, align_bytes=64)
        x_scales = keep.tile([P, HALVES, PASSES, HALF], U8, align_bytes=64)
        w_codes = keep.tile([P, PASSES, GATES], U32, align_bytes=64)
        w_scales = keep.tile([P, PASSES, GATES], U8, align_bytes=64)

        nc.vector.memset(bias_rows[:].bitcast(F32), 0.0)
        nc.vector.memset(warm[:], 0.0)
        make_identity(nc, ident_f[:])
        make_identity(nc, ident_bf[:])

        def load_bias(engine, first_row, vec):
            n = vec.shape[0] // P
            engine.dma_start(
                out=bias_rows[first_row : first_row + n, :], in_=vec.rearrange("(t n) -> t n", n=P)
            )

        load_bias(nc.scalar, 0, bias_ih)
        load_bias(nc.scalar, 32, bias_hh)
        for j, b in enumerate((bias_sh0, bias_sh1, bias_sh2)):
            load_bias(nc.gpsimd, 32 + CORE_TILES + 2 * j, b)
        nc.scalar.activation(out=warm[:], in_=warm[:], func=ACT.Sigmoid)
        nc.gpsimd.dma_start(out=mask_bf[:], in_=mask.rearrange("(p r) -> p r", r=ROW_TILES))

        w_rows_of = {}
        x_rows_of = {}

        def row_pair():
            return stage.tile([P, PAIR, DI], BF16, name="rows", bufs=ROW_BUFS)

        def load_weight_pair(q):
            w_rows_of[q] = row_pair()
            nc.sync.dma_start(
                out=w_rows_of[q][:],
                in_=weight_ih[PAIR * q * P : PAIR * (q + 1) * P, :].rearrange("(t p) k -> p t k", p=P),
            )

        def load_x_pair(q):
            x_rows_of[q] = row_pair()
            nc.sync.dma_start(out=x_rows_of[q][:], in_=x_view[:, PAIR * q : PAIR * (q + 1), :])

        def load_acts(first, count, which):
            rows = slice(first, first + count)
            for s in which:
                nc.sync.dma_start(out=acts_sb[:, s, rows, :], in_=act_views[s][:, rows, :])

        def load_c(first, count):
            rows = slice(first, first + count)
            nc.sync.dma_start(out=c_sb[:, rows, :], in_=c_view[:, rows, :])

        def load_plain_weight(t0, w):
            n = w.shape[0] // P
            nc.sync.dma_start(
                out=wplain_sb[:, t0 : t0 + n, :], in_=w.rearrange("(t p) k -> p t k", p=P)
            )

        H, S0, S1, S2 = range(4)
        load_x_pair(0)
        load_plain_weight(0, weight_hh)
        load_weight_pair(0)
        load_x_pair(1)
        for q in range(1, 4):
            load_weight_pair(q)
        load_acts(0, TILES_PER_HALF, (H,))
        load_c(0, TILES_PER_HALF)

        def copy_out(engine, out, in_):
            if engine == SCALAR:
                nc.scalar.copy(out=out, in_=in_)
            else:
                nc.vector.tensor_copy(out=out, in_=in_)

        def plain_weights(t0, count, engine):
            bank = psum.tile([P, 4, P], F32, name="bank_w", tag="bank")
            words = wplain_sb[:].bitcast(F32)
            for t in range(count):
                nc.tensor.transpose(bank[:, t, :], words[:, t0 + t, :], ident_f[:])
            pairs = bank[:, 0:count, :].rearrange("p t n -> p (t n)").bitcast(BF16)
            copy_out(
                engine,
                wplain_t[:, :, t0 * P : (t0 + count) * P],
                pairs.rearrange("p (n e) -> p e n", e=2),
            )

        acts_t_of = {}

        def prepare_acts(r, which, engine):
            if r not in acts_t_of:
                acts_t_of[r] = stage.tile([P, 4, P, 2], BF16, name="acts_t", bufs=3)
            words = acts_sb[:].bitcast(F32)
            bank = psum.tile([P, 4, P], F32, name="bank_a", tag="bank")
            for j, s in enumerate(which):
                nc.tensor.transpose(bank[:, j, :], words[:, s, r, :], ident_f[:])
            out = acts_t_of[r][:].rearrange("p s b e -> p s (b e)").bitcast(F32)
            copy_out(engine, out[:, which[0] : which[-1] + 1, :], bank[:, 0 : len(which), :])

        def transpose_bias():
            bank = psum.tile([P, P], BF16, name="bank_b", tag="bank")
            nc.tensor.transpose(bank[:], bias_rows[:], ident_bf[:])
            nc.vector.tensor_copy(out=bias_cols[:], in_=bank[:, 0:64])
            nc.vector.tensor_tensor(
                out=bias[:], in0=bias_cols[:, 0:W_TILES], in1=bias_cols[:, 32 : 32 + W_TILES], op=ALU.add
            )

        def regroup(engine, rows_bf16, grouped_words):
            words = rows_bf16.bitcast(F32)
            bank = psum.tile([P, PASSES, 2, P], F32, name="bank_q", tag="bank")
            for g in range(PASSES):
                for u in range(2):
                    nc.tensor.transpose(
                        bank[:, g, u, :], words[:, 2 * P * g + u : 2 * P * (g + 1) : 2], ident_f[:]
                    )
            copy_out(engine, grouped_words, bank[:].rearrange("p g u n -> p g n u"))

        def quantise(grouped, codes, scales):
            for g in range(PASSES):
                nc.vector.quantize_mx(
                    out=codes[:, g, :].bitcast(FP8X4),
                    scales=scales[:, g, :],
                    in_=grouped[:, g, :, :].rearrange("p n t -> p (n t)"),
                )

        def tile_of_pair(grouped, i):
            return grouped[:].bitcast(F32)[:, :, i * P : (i + 1) * P, :]

        w_grouped_of = {}
        x_grouped_of = {}

        def grouped_pair():
            return stage.tile([P, PASSES, PAIR * P, 4], BF16, align_bytes=64, name="grouped", bufs=GROUP_BUFS)

        def prepare_weights(t, engine):
            q, i = divmod(t, PAIR)
            if i == 0:
                w_grouped_of[q] = grouped_pair()
            regroup(engine, w_rows_of[q][:, i, :], tile_of_pair(w_grouped_of[q], i))

        def quantise_weights(q):
            cols = slice(PAIR * P * q, PAIR * P * (q + 1))
            quantise(w_grouped_of[q], w_codes[:, :, cols], w_scales[:, :, cols])

        def prepare_x(r, engine):
            q, i = divmod(r, PAIR)
            if i == 0:
                x_grouped_of[q] = grouped_pair()
            regroup(engine, x_rows_of[q][:, i, :], tile_of_pair(x_grouped_of[q], i))

        def quantise_x(q):
            half, i = divmod(q, TILES_PER_HALF // PAIR)
            cols = slice(PAIR * P * i, PAIR * P * (i + 1))
            quantise(x_grouped_of[q], x_codes[:, half, :, cols], x_scales[:, half, :, cols])

        mx_of = {}

        def mx(t, half):
            engine = SCALAR if t % 2 == 0 else VECTOR
            acc = psum.tile([P, HALF], F32, name="acc_mx", tag="bank")
            rows = slice(t * P, (t + 1) * P)
            for g in range(PASSES):
                nc.tensor.matmul_mx(
                    out=acc[:],
                    lhsT=w_codes[:, g, rows].bitcast(FP8X4),
                    lhsT_scale=w_scales[:, g, rows],
                    rhs=x_codes[:, half, g, :].bitcast(FP8X4),
                    rhs_scale=x_scales[:, half, g, :],
                    start=(g == 0),
                    stop=(g == PASSES - 1),
                )
            mx_of[t, half] = stage.tile([P, HALF], F32, name="mx_t%d" % t)
            out = mx_of[t, half][:]
            if engine == SCALAR:
                nc.scalar.activation(out=out, in_=acc[:], func=ACT.Identity, bias=bias[:, t : t + 1])
            else:
                nc.vector.tensor_scalar(out=out, in0=acc[:], scalar1=bias[:, t : t + 1], scalar2=None, op0=ALU.add)

        gates_of = {}

        def parts(r, names):
            half, i = divmod(r, TILES_PER_HALF)
            accs = {}
            for name in names:
                accs[name] = psum.tile([P, HALF], F32, name="acc_part", tag="bank")
                tiles = [g0 // P + j for g0, width, s in PARTS[name] for j in range(width // P)]
                for at, t in enumerate(tiles):
                    nc.tensor.matmul(
                        accs[name][:, at * P : (at + 1) * P],
                        lhsT=mx_of[t, half][:, i * P : (i + 1) * P],
                        rhs=ident_f[:],
                        is_transpose=True,
                        start=(at == 0),
                        stop=False,
                    )
            for name in names:
                at = 0
                runs = PARTS[name]
                for g0, width, s in runs:
                    for e in range(2):
                        nc.tensor.matmul(
                            accs[name][:, at : at + width],
                            lhsT=acts_t_of[r][:, s, :, e],
                            rhs=wplain_t[:, e, g0 : g0 + width],
                            start=False,
                            stop=(e == 1 and g0 == runs[-1][0]),
                        )
                    at += width
            return accs

        I, F, O, C_HAT, MC, B0, B1, B2 = range(8)

        def gate(r, first, count=1):
            return gates_of[r][:, first : first + count, :]

        def new_gates(r):
            gates_of[r] = gate_pool.tile([P, 8, DH], F32, name="gates")

        def squash(r, *names):
            accs = parts(r, names)
            gates_and_func = {
                "i f": (gate(r, I, 2), ACT.Sigmoid),
                "c_hat": (gate(r, C_HAT), ACT.Tanh),
                "o b2": (gates_of[r][:, O : B2 + 1 : B2 - O, :], ACT.Sigmoid),
                "b0 b1": (gate(r, B0, 2), ACT.Sigmoid),
            }
            for name in names:
                gates, func = gates_and_func[name]
                width = sum(run[1] for run in PARTS[name])
                nc.scalar.activation(
                    out=gates, in_=accs[name][:, 0:width].rearrange("p (k d) -> p k d", d=DH), func=func
                )

        def row_mask(r):
            return mask_f[:, r : r + 1]

        def mask_c(r):
            nc.scalar.activation(
                out=gate(r, MC), in_=c_sb[:, r : r + 1, :], func=ACT.Copy, scale=row_mask(r)
            )

        prod_of = {}
        outs_of = {}
        t_cell_of = {}
        e_of = {}

        def products(r):
            prod_of[r] = work.tile([P, 2, DH], F32, name="prod")
            nc.vector.tensor_tensor(
                out=prod_of[r][:], in0=gate(r, I, 2), in1=gate(r, C_HAT, 2), op=ALU.mult
            )

        def store(r, k):
            nc.sync.dma_start(out=out_views[k][:, r, :], in_=outs_of[r][:, k, :])

        def cell(r):
            outs_of[r] = work.tile([P, 5, DH], F32, name="outs", bufs=4)
            nc.vector.scalar_tensor_tensor(
                out=outs_of[r][:, 1, :], in0=prod_of[r][:, 0, :], scalar=row_mask(r),
                in1=prod_of[r][:, 1, :], op0=ALU.mult, op1=ALU.add,
            )
            store(r, 1)

        def tanh_cell(r):
            t_cell_of[r] = work.tile([P, DH], F32, name="t_cell", bufs=4)
            t_cell = t_cell_of[r][:]
            nc.scalar.activation(out=t_cell, in_=outs_of[r][:, 1, :], func=ACT.Tanh)
            nc.scalar.activation(out=t_cell, in_=t_cell, func=ACT.Copy, scale=row_mask(r))

        def minus_o(r):
            b = gate(r, B0, 3)
            nc.vector.tensor_tensor(
                out=b, in0=b, in1=gate(r, O).to_broadcast([P, 3, DH]), op=ALU.subtract
            )

        def hidden(r):
            nc.vector.tensor_tensor(
                out=outs_of[r][:, 0, :], in0=gates_of[r][:, O, :], in1=t_cell_of[r][:], op=ALU.mult
            )
            store(r, 0)

        def finish(r, *steps):
            stt = nc.vector.scalar_tensor_tensor
            t_cell = t_cell_of[r][:]
            s0_out, s1_out, s2_out = [outs_of[r][:, k, :] for k in (2, 3, 4)]
            if r not in e_of:
                e_of[r] = (work.tile([P, DH], F32, name="e1"), work.tile([P, DH], F32, name="e2"))
            e1, e2 = [e[:] for e in e_of[r]]
            b0, b1, b2 = [gates_of[r][:, b, :] for b in (B0, B1, B2)]
            for step in steps:
                if step == 0:
                    stt(out=s0_out, in0=b0, scalar=1.0, in1=t_cell, op0=ALU.add, op1=ALU.mult)
                    store(r, 2)
                if step == 1:
                    stt(out=e1, in0=b1, scalar=2.0, in1=s0_out, op0=ALU.add, op1=ALU.subtract)
                if step == 2:
                    stt(out=e2, in0=s0_out, scalar=-2.0, in1=b2, op0=ALU.mult, op1=ALU.add)
                if step == 3:
                    stt(out=s1_out, in0=e1, scalar=0.5, in1=t_cell, op0=ALU.mult, op1=ALU.mult)
                    store(r, 3)
                if step == 4:
                    stt(out=e2, in0=e2, scalar=3.0, in1=s1_out, op0=ALU.add, op1=ALU.subtract)
                if step == 5:
                    stt(out=s2_out, in0=e2, scalar=1.0 / 3.0, in1=t_cell, op0=ALU.mult, op1=ALU.mult)
                    store(r, 4)

        def core_gates(r):
            new_gates(r)
            mask_c(r)
            squash(r, "i f", "c_hat")

        def shared_gates(r):
            squash(r, "b0 b1", "o b2")

        def begin_outputs(r):
            finish(r, 0)
            hidden(r)

        prepare_x(0, VECTOR)
        prepare_x(1, VECTOR)
        quantise_x(0)
        load_weight_pair(4)
        plain_weights(0, 4, SCALAR)
        plain_weights(4, 4, SCALAR)
        prepare_weights(0, SCALAR)
        prepare_x(2, VECTOR)
        prepare_x(3, VECTOR)
        quantise_x(1)
        prepare_weights(1, SCALAR)
        load_weight_pair(5)
        quantise_weights(0)
        prepare_weights(2, SCALAR)
        prepare_weights(3, SCALAR)
        load_weight_pair(6)
        load_acts(0, TILES_PER_HALF, (S0, S1, S2))
        for j, w in enumerate((weight_sh0, weight_sh1, weight_sh2)):
            load_plain_weight(CORE_TILES + 2 * j, w)
        quantise_weights(1)
        prepare_weights(4, SCALAR)
        prepare_weights(5, SCALAR)
        load_x_pair(2)
        load_x_pair(3)
        load_acts(TILES_PER_HALF, TILES_PER_HALF, (H, S0, S1, S2))
        load_c(TILES_PER_HALF, TILES_PER_HALF)
        quantise_weights(2)
        transpose_bias()
        prepare_weights(6, SCALAR)
        for t in range(6):
            mx(t, 0)
        prepare_weights(7, SCALAR)
        quantise_weights(3)
        nc.vector.tensor_copy(out=mask_f[:], in_=mask_bf[:])
        prepare_acts(0, (H,), SCALAR)
        prepare_acts(1, (H,), SCALAR)

        new_gates(0)
        mask_c(0)
        prepare_weights(8, SCALAR)
        squash(0, "i f")
        mx(6, 0)
        mx(7, 0)
        prepare_weights(9, SCALAR)
        quantise_weights(4)
        prepare_weights(10, SCALAR)
        prepare_weights(11, SCALAR)
        squash(0, "c_hat")
        prepare_weights(12, SCALAR)
        quantise_weights(5)
        products(0)
        prepare_weights(13, SCALAR)
        cell(0)
        quantise_weights(6)
        plain_weights(CORE_TILES, 4, VECTOR)
        plain_weights(CORE_TILES + 4, 2, SCALAR)
        prepare_acts(0, (S0, S1, S2), SCALAR)
        mx(8, 0)
        mx(9, 0)
        prepare_acts(2, (H, S0, S1, S2), SCALAR)
        tanh_cell(0)
        prepare_acts(1, (S0, S1, S2), SCALAR)
        new_gates(1)
        mask_c(1)
        squash(1, "i f")
        for t in range(10, W_TILES):
            mx(t, 0)
        squash(1, "c_hat")
        products(1)
        cell(1)
        shared_gates(0)
        minus_o(0)
        shared_gates(1)
        prepare_acts(3, (H, S0, S1, S2), SCALAR)

        for half in range(HALVES):
            first = half * TILES_PER_HALF
            last = first + TILES_PER_HALF - 1
            for n in range(first + 2 if half == 0 else first, last + 3):
                making = n <= last
                finishing = n - 2 >= first
                if making:
                    core_gates(n)
                if first <= n - 1 <= last:
                    tanh_cell(n - 1)
                if making:
                    shared_gates(n)
                if n == 2:
                    for r in range(TILES_PER_HALF, ROW_TILES):
                        prepare_x(r, SCALAR)
                if n == TILES_PER_HALF and half == 0:
                    for t in range(3):
                        mx(t, 1)
                if making and n + 2 < ROW_TILES:
                    prepare_acts(n + 2, (H, S0, S1, S2), SCALAR)
                if finishing:
                    if n - 2 < last:
                        begin_outputs(n - 2)
                    finish(n - 2, 1, 2, 3)
                if n == TILES_PER_HALF and half == 0:
                    for t in range(3, 7):
                        mx(t, 1)
                if first <= n - 1 <= last and n > 2:
                    minus_o(n - 1)
                if finishing:
                    finish(n - 2, 4)
                if n - 1 == last:
                    begin_outputs(last)
                if making:
                    products(n)
                if finishing:
                    finish(n - 2, 5)
                if making:
                    cell(n)
                if n == 2:
                    minus_o(1)
                    quantise_x(2)
                    quantise_x(3)
                if n == TILES_PER_HALF and half == 0:
                    for t in range(7, W_TILES):
                        mx(t, 1)
